import numpy as np
import ml_dtypes


def mxq(x, axis, fmt="e4m3"):
    dtype, down = {"e4m3": (ml_dtypes.float8_e4m3fn, 7), "e5m2": (ml_dtypes.float8_e5m2, 14)}[fmt]
    v = np.moveaxis(np.asarray(x, np.float32).astype(ml_dtypes.bfloat16).astype(np.float64), axis, -1)
    blocks = v.reshape(v.shape[:-1] + (-1, 32))
    amax = np.abs(blocks).max(-1, keepdims=True)
    byte = np.maximum(np.where(amax > 0, np.frexp(amax)[1] - 1 + 127, 0) - down, 1)
    scale = np.exp2(byte - 127.0)
    codes = (blocks / scale).astype(np.float32).astype(dtype).astype(np.float64)
    return np.moveaxis((codes * scale).reshape(v.shape), -1, axis)


WIDE = False


def mx_kscale(k):
    if not WIDE:
        return np.ones(k)
    levels = np.array([10, -10, 5, -5, 0])
    a = np.random.permutation(np.resize(levels, k // 512 * 4)).reshape(k // 512, 4)
    idx = np.arange(k)
    return np.exp2(a[idx // 512, idx % 128 // 32])


BF16 = ml_dtypes.bfloat16


def bf(x):
    return np.asarray(x, np.float32).astype(BF16)


def f64(x):
    return np.asarray(x).astype(np.float64)


B, S, HID, NH, DH, CHUNK = 1, 4096, 1024, 2, 128, 512
W = NH * DH
NC = S // CHUNK


def chunks(x):
    return x.reshape(B, S, NH, DH).transpose(0, 2, 1, 3).reshape(B, NH, NC, CHUNK, DH)


def with_prev(own, prev, op):
    return np.concatenate([own[:, :, :1], op(own[:, :, 1:], prev)], axis=2)


def setup_inputs():
    s = mx_kscale(HID)
    return {"q": bf(np.random.standard_normal((B, S, W)) * np.sqrt(2.0)),
            "k_scaled": bf(np.random.standard_normal((B, S, W)) * np.sqrt(2.0 / DH)),
            "hidden_states": bf(np.random.standard_normal((B, S, HID)) * s),
            "Wv": bf(np.random.standard_normal((HID, W)) / np.sqrt(HID) / s[:, None])}


def reference(q, k_scaled, hidden_states, Wv):
    q5, k5 = chunks(f64(q)), chunks(f64(k_scaled))
    v = mxq(f64(hidden_states), 2, "e4m3") @ mxq(f64(Wv), 0, "e4m3")
    vq = mxq(chunks(v), 3, "e4m3")
    pos = np.arange(CHUNK)
    later = np.where(pos[:, None] < pos[None, :], 1e9, 0.0)
    d_own = q5 @ k5.transpose(0, 1, 2, 4, 3) - later
    d_prev = q5[:, :, 1:] @ k5[:, :, :-1].transpose(0, 1, 2, 4, 3)
    m = with_prev(d_own.max(-1, keepdims=True), d_prev.max(-1, keepdims=True), np.maximum)
    e_own = np.exp(d_own - m)
    e_prev = np.exp(d_prev - m[:, :, 1:])
    den = with_prev(e_own.sum(-1, keepdims=True), e_prev.sum(-1, keepdims=True), np.add)
    num = with_prev(mxq(e_own, 4, "e4m3") @ vq, mxq(e_prev, 4, "e4m3") @ vq[:, :, :-1], np.add)
    res = num / den
    return res.reshape(B, NH, S, DH).transpose(0, 2, 1, 3).reshape(B, S, W)

@@ -1,0 +1,284 @@
+from contextlib import ExitStack
+
+import concourse.mybir as mybir
+from concourse.masks import make_identity
+
+F32 = mybir.dt.float32
+BF16 = mybir.dt.bfloat16
+U32 = mybir.dt.uint32
+U8 = mybir.dt.uint8
+FP8X4 = mybir.dt.float8_e4m3fn_x4
+ACT = mybir.ActivationFunctionType
+ALU = mybir.AluOpType
+AXIS = mybir.AxisListType
+
+P = 128
+PACK = 4
+SEQ = 4096
+HID = 1024
+HEADS = 2
+DH = 128
+WIDTH = HEADS * DH
+CHUNK = 512
+N_CHUNKS = SEQ // CHUNK
+TILES = CHUNK // P
+HID_PASSES = HID // CHUNK
+MASKED = -1.0e9
+
+SCORE_CELLS = HEADS * (2 * N_CHUNKS - 1) * CHUNK * CHUNK
+FLOPS = 2 * SEQ * HID * WIDTH + 2 * 2 * SCORE_CELLS * DH
+
+
+def tile_localselfattention_pa_t_kernel(tc, q, k_scaled, hidden_states, Wv, out):
+    nc = tc.nc
+    q_rows = q.flatten_outer_dims().rearrange("(c i p) w -> c p i w", i=TILES, p=P)
+    k_rows = k_scaled.flatten_outer_dims().rearrange("(c i p) w -> c p i w", i=TILES, p=P)
+    h_rows = hidden_states.flatten_outer_dims().rearrange("(c t p) k -> c p t k", t=TILES, p=P)
+    out_rows = out.flatten_outer_dims().rearrange("(n p) w -> n p w", p=P)
+
+    with ExitStack() as ctx:
+        const = ctx.enter_context(tc.tile_pool(name="const", bufs=1))
+        raw = ctx.enter_context(tc.tile_pool(name="raw", bufs=1))
+        work = ctx.enter_context(tc.tile_pool(name="work", bufs=2))
+        score_psum = ctx.enter_context(tc.psum_pool(name="score_psum", bufs=2))
+        flip_psum = ctx.enter_context(tc.psum_pool(name="flip_psum", bufs=2))
+        sum_psum = ctx.enter_context(tc.psum_pool(name="sum_psum", bufs=1))
+        prep_psum = ctx.enter_context(tc.psum_pool(name="prep_psum", bufs=1))
+
+        q_raw, k_raw, h_raw = {}, {}, {}
+        w_raw = raw.tile([P, HID_PASSES * PACK * WIDTH], BF16)
+        for c in range(N_CHUNKS):
+            k_raw[c] = raw.tile([P, TILES, WIDTH], BF16, name="k_raw%d" % c)
+            nc.sync.dma_start(out=k_raw[c][:], in_=k_rows[c])
+            q_raw[c] = raw.tile([P, TILES, WIDTH], BF16, name="q_raw%d" % c)
+            nc.sync.dma_start(out=q_raw[c][:], in_=q_rows[c])
+            if c == 0:
+                nc.sync.dma_start(
+                    out=w_raw[:].rearrange("p (s x) -> p s x", s=HID_PASSES * 2),
+                    in_=Wv.rearrange("(s p e) n -> p s (e n)", p=P, e=2),
+                )
+            h_raw[c] = raw.tile([P, TILES * HID], BF16, name="h_raw%d" % c)
+            nc.sync.dma_start(out=h_raw[c][:].rearrange("p (t k) -> p t k", t=TILES), in_=h_rows[c])
+
+        ident_bf = const.tile([P, P], BF16)
+        make_identity(nc, ident_bf[:])
+        ident_f32 = const.tile([P, P], F32)
+        make_identity(nc, ident_f32[:])
+        mask_f32 = const.tile([P, P], F32)
+        nc.gpsimd.memset(mask_f32[:], 0.0)
+        nc.gpsimd.affine_select(
+            out=mask_f32[:], in_=mask_f32[:], compare_op=ALU.is_ge, fill=MASKED,
+            base=0, pattern=[[-1, P]], channel_multiplier=1,
+        )
+        mask_bf = const.tile([P, P], BF16)
+        nc.vector.tensor_copy(out=mask_bf[:], in_=mask_f32[:])
+        zero_block = const.tile([P, P], BF16)
+        nc.vector.memset(zero_block[:], 0.0)
+
+        w_grp = const.tile([P, HID_PASSES * WIDTH * PACK], BF16, align_bytes=64)
+        w_codes = const.tile([P, HID_PASSES * WIDTH], U32, align_bytes=64)
+        w_scales = const.tile([P, HID_PASSES * WIDTH], U8, align_bytes=64)
+        nc.vector.tensor_copy(
+            out=w_grp[:].rearrange("p (g n t) -> p g n t", g=HID_PASSES, t=PACK),
+            in_=w_raw[:].rearrange("p (g t n) -> p g n t", g=HID_PASSES, t=PACK),
+        )
+        nc.vector.quantize_mx(out=w_codes[:].bitcast(FP8X4), scales=w_scales[:], in_=w_grp[:])
+
+        k_t, q_t, h_grp, h_codes, h_scales, v_grp, v_codes, v_scales = {}, {}, {}, {}, {}, {}, {}, {}
+        prep_bank = {}
+
+        def prepare_on_tensor(c, piece):
+            if piece < 2:
+                src = k_raw[c] if piece == 0 else q_raw[c]
+                bank = prep_psum.tile([P, HEADS, TILES, P], BF16, tag="prep", name="qk_bank")
+                for h in range(HEADS):
+                    for i in range(TILES):
+                        nc.tensor.transpose(bank[:, h, i, :], src[:, i, h * DH:(h + 1) * DH], ident_bf[:])
+            elif piece < 2 + TILES:
+                t = piece - 2
+                words = h_raw[c][:].bitcast(F32)
+                bank = prep_psum.tile([P, HID_PASSES, 2, P], F32, tag="prep", name="h_bank")
+                for g in range(HID_PASSES):
+                    for a in range(2):
+                        first = (t * HID_PASSES * 2 + g * 2 + a) * P
+                        nc.tensor.transpose(bank[:, g, a, :], words[:, first:first + P], ident_f32[:])
+            else:
+                h = piece - 2 - TILES
+                bank = prep_psum.tile([P, TILES, DH], F32, tag="prep", name="v_bank")
+                for t in range(TILES):
+                    for g in range(HID_PASSES):
+                        rows = slice((t * HID_PASSES + g) * P, (t * HID_PASSES + g + 1) * P)
+                        cols = slice(g * WIDTH + h * DH, g * WIDTH + (h + 1) * DH)
+                        nc.tensor.matmul_mx(
+                            out=bank[:, t, :],
+                            lhsT=h_codes[c][:, rows].bitcast(FP8X4), lhsT_scale=h_scales[c][:, rows],
+                            rhs=w_codes[:, cols].bitcast(FP8X4), rhs_scale=w_scales[:, cols],
+                            start=(g == 0), stop=(g == HID_PASSES - 1),
+                        )
+            prep_bank[(c, piece)] = bank
+
+        def prepare_on_vector(c, piece):
+            bank = prep_bank[(c, piece)]
+            if piece < 2:
+                flipped = work.tile([P, HEADS, CHUNK], BF16, tag="k_t" if piece == 0 else "q_t",
+                                    bufs=3 if piece == 0 else 2, name="flipped")
+                nc.vector.tensor_copy(out=flipped[:], in_=bank[:].rearrange("p h i x -> p h (i x)"))
+                if piece == 0:
+                    k_t[c] = flipped
+                else:
+                    q_t[c] = flipped
+            elif piece < 2 + TILES:
+                t = piece - 2
+                if t == 0:
+                    h_grp[c] = work.tile([P, TILES * HID_PASSES * P * PACK], BF16, align_bytes=64, name="h_grp")
+                    h_codes[c] = work.tile([P, TILES * HID_PASSES * P], U32, align_bytes=64, name="h_codes")
+                    h_scales[c] = work.tile([P, TILES * HID_PASSES * P], U8, align_bytes=64, name="h_scales")
+                grouped = h_grp[c][:].bitcast(F32).rearrange(
+                    "p (t g x a) -> p t g x a", t=TILES, g=HID_PASSES, a=2)
+                nc.vector.tensor_copy(out=grouped[:, t], in_=bank[:].rearrange("p g a x -> p g x a"))
+                words = slice(t * HID_PASSES * P, (t + 1) * HID_PASSES * P)
+                nc.vector.quantize_mx(
+                    out=h_codes[c][:, words].bitcast(FP8X4), scales=h_scales[c][:, words],
+                    in_=h_grp[c][:, t * HID_PASSES * P * PACK:(t + 1) * HID_PASSES * P * PACK],
+                )
+            else:
+                h = piece - 2 - TILES
+                if h == 0:
+                    v_grp[c] = work.tile([P, WIDTH * PACK], BF16, align_bytes=64, name="v_grp")
+                    v_codes[c] = work.tile([P, WIDTH], U32, align_bytes=64, bufs=3, name="v_codes")
+                    v_scales[c] = work.tile([P, WIDTH], U8, align_bytes=64, bufs=3, name="v_scales")
+                nc.vector.tensor_copy(
+                    out=v_grp[c][:, h * DH * PACK:(h + 1) * DH * PACK].rearrange("p (d t) -> p d t", t=PACK),
+                    in_=bank[:].rearrange("p t d -> p d t"),
+                )
+                if h == HEADS - 1:
+                    nc.vector.quantize_mx(out=v_codes[c][:].bitcast(FP8X4), scales=v_scales[c][:], in_=v_grp[c][:])
+
+        units = [(c, i, h) for c in range(N_CHUNKS) for i in range(TILES) for h in range(HEADS)]
+        s_own, s_prev, neg_max, e_rows, e_bank, e_grp, e_codes, e_scales = {}, {}, {}, {}, {}, {}, {}, {}
+        row_sums, acc = {}, {}
+
+        def scores(u):
+            c, i, h = units[u]
+            seen = (i + 1) * P
+            queries = q_t[c][:, h, i * P:(i + 1) * P]
+            s_own[u] = score_psum.tile([P, CHUNK], F32, name="s_own")
+            nc.tensor.matmul(s_own[u][:, :seen], lhsT=queries, rhs=k_t[c][:, h, :seen], start=True, stop=False)
+            nc.tensor.matmul(s_own[u][:, i * P:seen], lhsT=ident_bf[:], rhs=mask_bf[:], start=False, stop=True)
+            if c > 0:
+                s_prev[u] = score_psum.tile([P, CHUNK], F32, name="s_prev")
+                nc.tensor.matmul(s_prev[u][:], lhsT=queries, rhs=k_t[c - 1][:, h, :], start=True, stop=True)
+
+        def maxima(u):
+            c, i, h = units[u]
+            seen = (i + 1) * P
+            neg_max[u] = work.tile([P, 1], F32, bufs=4, name="neg_max")
+            if c == 0:
+                nc.vector.tensor_reduce(out=neg_max[u][:], in_=s_own[u][:, :seen], axis=AXIS.X, op=ALU.max, negate=True)
+            else:
+                both = work.tile([P, 2], F32, bufs=4, name="both")
+                nc.vector.tensor_reduce(out=both[:, 0:1], in_=s_own[u][:, :seen], axis=AXIS.X, op=ALU.max)
+                nc.vector.tensor_reduce(out=both[:, 1:2], in_=s_prev[u][:], axis=AXIS.X, op=ALU.max)
+                nc.vector.tensor_reduce(out=neg_max[u][:], in_=both[:], axis=AXIS.X, op=ALU.max, negate=True)
+
+        def exponentials(u):
+            c, i, h = units[u]
+            seen = (i + 1) * P
+            if h == 0:
+                row_sums[(c, i)] = work.tile([P, HEADS, 2], F32, bufs=4, name="row_sums")
+            sums = row_sums[(c, i)]
+            e_rows[u] = work.tile([P, 2 * CHUNK], BF16, bufs=3, name="e_rows")
+            nc.scalar.activation(out=e_rows[u][:, :seen], in_=s_own[u][:, :seen], func=ACT.Exp,
+                                 bias=neg_max[u][:], scale=1.0, accum_out=sums[:, h, 0:1])
+            if c > 0:
+                nc.scalar.activation(out=e_rows[u][:, CHUNK:], in_=s_prev[u][:], func=ACT.Exp,
+                                     bias=neg_max[u][:], scale=1.0, accum_out=sums[:, h, 1:2])
+
+        def flip(u):
+            c, i, h = units[u]
+            e_bank[u] = flip_psum.tile([P, 2, PACK, P], BF16, name="e_bank")
+            for t in range(PACK):
+                block = e_rows[u][:, t * P:(t + 1) * P] if t <= i else zero_block[:]
+                nc.tensor.transpose(e_bank[u][:, 0, t, :], block, ident_bf[:])
+            if c > 0:
+                for t in range(PACK):
+                    nc.tensor.transpose(e_bank[u][:, 1, t, :], e_rows[u][:, CHUNK + t * P:CHUNK + (t + 1) * P], ident_bf[:])
+
+        def regroup(u):
+            c, i, h = units[u]
+            sides = 1 if c == 0 else 2
+            e_grp[u] = work.tile([P, 2 * CHUNK], BF16, align_bytes=64, bufs=3, name="e_grp")
+            nc.scalar.copy(
+                out=e_grp[u][:, :sides * CHUNK].rearrange("p (s x t) -> p s x t", s=sides, t=PACK),
+                in_=e_bank[u][:, :sides].rearrange("p s t x -> p s x t"),
+            )
+
+        def quantise(u):
+            c, i, h = units[u]
+            sides = 1 if c == 0 else 2
+            e_codes[u] = work.tile([P, 2 * P], U32, align_bytes=64, bufs=3, name="e_codes")
+            e_scales[u] = work.tile([P, 2 * P], U8, align_bytes=64, bufs=3, name="e_scales")
+            nc.vector.quantize_mx(out=e_codes[u][:, :sides * P].bitcast(FP8X4), scales=e_scales[u][:, :sides * P],
+                                  in_=e_grp[u][:, :sides * CHUNK])
+
+        def weighted_sum(u):
+            c, i, h = units[u]
+            if h == 0:
+                acc[(c, i)] = sum_psum.tile([P, HEADS, DH], F32, name="acc")
+            cols = slice(h * DH, (h + 1) * DH)
+            nc.tensor.matmul_mx(
+                out=acc[(c, i)][:, h, :],
+                lhsT=e_codes[u][:, :P].bitcast(FP8X4), lhsT_scale=e_scales[u][:, :P],
+                rhs=v_codes[c][:, cols].bitcast(FP8X4), rhs_scale=v_scales[c][:, cols],
+                start=True, stop=(c == 0),
+            )
+            if c > 0:
+                nc.tensor.matmul_mx(
+                    out=acc[(c, i)][:, h, :],
+                    lhsT=e_codes[u][:, P:].bitcast(FP8X4), lhsT_scale=e_scales[u][:, P:],
+                    rhs=v_codes[c - 1][:, cols].bitcast(FP8X4), rhs_scale=v_scales[c - 1][:, cols],
+                    start=False, stop=True,
+                )
+
+        def finish(c, i):
+            inverse = work.tile([P, HEADS], F32, bufs=4, name="inverse")
+            if c == 0:
+                nc.vector.reciprocal(out=inverse[:], in_=row_sums[(c, i)][:, :, 0])
+            else:
+                total = work.tile([P, HEADS], F32, bufs=4, name="total")
+                nc.vector.tensor_reduce(out=total[:], in_=row_sums[(c, i)][:], axis=AXIS.X, op=ALU.add)
+                nc.vector.reciprocal(out=inverse[:], in_=total[:])
+            result = work.tile([P, WIDTH], F32, bufs=4, name="result")
+            for h in range(HEADS):
+                nc.scalar.activation(out=result[:, h * DH:(h + 1) * DH], in_=acc[(c, i)][:, h, :], func=ACT.Copy,
+                                     scale=inverse[:, h:h + 1])
+            nc.sync.dma_start(out=out_rows[c * TILES + i], in_=result[:])
+
+        pieces = 2 + TILES + HEADS
+        assert pieces == TILES * HEADS
+        for piece in range(pieces):
+            prepare_on_tensor(0, piece)
+            prepare_on_vector(0, piece)
+
+        n = len(units)
+        for k in range(-1, n + 3):
+            if 0 <= k - 3 and units[k - 3][2] == HEADS - 1:
+                finish(units[k - 3][0], units[k - 3][1])
+            if 0 <= k - 2 < n:
+                quantise(k - 2)
+            if 1 <= k < n + 1 and (k - 1) // pieces + 1 < N_CHUNKS:
+                prepare_on_vector((k - 1) // pieces + 1, (k - 1) % pieces)
+            if 0 <= k - 1 < n:
+                flip(k - 1)
+            if 0 <= k < n:
+                exponentials(k)
+            if k + 1 < n:
+                scores(k + 1)
+            if 0 <= k - 1 < n:
+                regroup(k - 1)
+            if 0 <= k - 2 < n:
+                weighted_sum(k - 2)
+            if 0 <= k < n and k // pieces + 1 < N_CHUNKS:
+                prepare_on_tensor(k // pieces + 1, k % pieces)
+            if k + 1 < n:
+                maxima(k + 1)

@@ -24,6 +24,7 @@ N_CHUNKS = SEQ // CHUNK
 TILES = CHUNK // P
 HID_PASSES = HID // CHUNK
 MASKED = -1.0e9
+LEAD = 7
 
 SCORE_CELLS = HEADS * (2 * N_CHUNKS - 1) * CHUNK * CHUNK
 FLOPS = 2 * SEQ * HID * WIDTH + 2 * 2 * SCORE_CELLS * DH
@@ -156,18 +157,22 @@ def tile_localselfattention_pa_t_kernel(tc, q, k_scaled, hidden_states, Wv, out)
 
         units = [(c, i, h) for c in range(N_CHUNKS) for i in range(TILES) for h in range(HEADS)]
         s_own, s_prev, neg_max, e_rows, e_bank, e_grp, e_codes, e_scales = {}, {}, {}, {}, {}, {}, {}, {}
-        row_sums, acc = {}, {}
+        row_sums, inverse, acc = {}, {}, {}
 
-        def scores(u):
+        def scores_own(u):
             c, i, h = units[u]
             seen = (i + 1) * P
             queries = q_t[c][:, h, i * P:(i + 1) * P]
             s_own[u] = score_psum.tile([P, CHUNK], F32, name="s_own")
             nc.tensor.matmul(s_own[u][:, :seen], lhsT=queries, rhs=k_t[c][:, h, :seen], start=True, stop=False)
             nc.tensor.matmul(s_own[u][:, i * P:seen], lhsT=ident_bf[:], rhs=mask_bf[:], start=False, stop=True)
+
+        def scores_prev(u):
+            c, i, h = units[u]
             if c > 0:
                 s_prev[u] = score_psum.tile([P, CHUNK], F32, name="s_prev")
-                nc.tensor.matmul(s_prev[u][:], lhsT=queries, rhs=k_t[c - 1][:, h, :], start=True, stop=True)
+                nc.tensor.matmul(s_prev[u][:], lhsT=q_t[c][:, h, i * P:(i + 1) * P], rhs=k_t[c - 1][:, h, :],
+                                 start=True, stop=True)
 
         def maxima(u):
             c, i, h = units[u]
@@ -240,45 +245,49 @@ def tile_localselfattention_pa_t_kernel(tc, q, k_scaled, hidden_states, Wv, out)
                     start=False, stop=True,
                 )
 
-        def finish(c, i):
-            inverse = work.tile([P, HEADS], F32, bufs=4, name="inverse")
+        def invert_sums(c, i):
+            inverse[(c, i)] = work.tile([P, HEADS], F32, bufs=4, name="inverse")
             if c == 0:
-                nc.vector.reciprocal(out=inverse[:], in_=row_sums[(c, i)][:, :, 0])
+                nc.vector.reciprocal(out=inverse[(c, i)][:], in_=row_sums[(c, i)][:, :, 0])
             else:
                 total = work.tile([P, HEADS], F32, bufs=4, name="total")
                 nc.vector.tensor_reduce(out=total[:], in_=row_sums[(c, i)][:], axis=AXIS.X, op=ALU.add)
-                nc.vector.reciprocal(out=inverse[:], in_=total[:])
+                nc.vector.reciprocal(out=inverse[(c, i)][:], in_=total[:])
+
+        def finish(c, i):
             result = work.tile([P, WIDTH], F32, bufs=4, name="result")
-            for h in range(HEADS):
-                nc.scalar.activation(out=result[:, h * DH:(h + 1) * DH], in_=acc[(c, i)][:, h, :], func=ACT.Copy,
-                                     scale=inverse[:, h:h + 1])
+            nc.vector.tensor_scalar(out=result[:, :DH], in0=acc[(c, i)][:, 0, :], scalar1=inverse[(c, i)][:, 0:1],
+                                    scalar2=None, op0=ALU.mult)
+            nc.scalar.activation(out=result[:, DH:], in_=acc[(c, i)][:, 1, :], func=ACT.Copy,
+                                 scale=inverse[(c, i)][:, 1:2])
             nc.sync.dma_start(out=out_rows[c * TILES + i], in_=result[:])
 
         pieces = 2 + TILES + HEADS
         assert pieces == TILES * HEADS
-        for piece in range(pieces):
-            prepare_on_tensor(0, piece)
-            prepare_on_vector(0, piece)
-
         n = len(units)
-        for k in range(-1, n + 3):
-            if 0 <= k - 3 and units[k - 3][2] == HEADS - 1:
-                finish(units[k - 3][0], units[k - 3][1])
-            if 0 <= k - 2 < n:
-                quantise(k - 2)
-            if 1 <= k < n + 1 and (k - 1) // pieces + 1 < N_CHUNKS:
-                prepare_on_vector((k - 1) // pieces + 1, (k - 1) % pieces)
-            if 0 <= k - 1 < n:
-                flip(k - 1)
-            if 0 <= k < n:
-                exponentials(k)
-            if k + 1 < n:
-                scores(k + 1)
-            if 0 <= k - 1 < n:
-                regroup(k - 1)
-            if 0 <= k - 2 < n:
-                weighted_sum(k - 2)
-            if 0 <= k < n and k // pieces + 1 < N_CHUNKS:
-                prepare_on_tensor(k // pieces + 1, k % pieces)
-            if k + 1 < n:
-                maxima(k + 1)
+        with tc.manual_schedule():
+            for k in range(-LEAD, n + 3):
+                if 0 <= k - 3 and units[k - 3][2] == HEADS - 1:
+                    finish(units[k - 3][0], units[k - 3][1])
+                if 0 <= k - 2 < n:
+                    quantise(k - 2)
+                if 0 <= k + LEAD - 1 < n:
+                    prepare_on_vector((k + LEAD - 1) // pieces, (k + LEAD - 1) % pieces)
+                if 0 <= k - 2 < n and units[k - 2][2] == HEADS - 1:
+                    invert_sums(units[k - 2][0], units[k - 2][1])
+                if 0 <= k - 1 < n:
+                    flip(k - 1)
+                if 0 <= k < n:
+                    exponentials(k)
+                if 0 <= k + 1 < n:
+                    scores_own(k + 1)
+                if 0 <= k - 1 < n:
+                    regroup(k - 1)
+                if 0 <= k - 2 < n:
+                    weighted_sum(k - 2)
+                if 0 <= k + 1 < n:
+                    scores_prev(k + 1)
+                if 0 <= k + LEAD < n:
+                    prepare_on_tensor((k + LEAD) // pieces, (k + LEAD) % pieces)
+                if 0 <= k + 1 < n:
+                    maxima(k + 1)

@@ -24,7 +24,7 @@ N_CHUNKS = SEQ // CHUNK
 TILES = CHUNK // P
 HID_PASSES = HID // CHUNK
 MASKED = -1.0e9
-LEAD = 7
+LEAD = 6
 
 SCORE_CELLS = HEADS * (2 * N_CHUNKS - 1) * CHUNK * CHUNK
 FLOPS = 2 * SEQ * HID * WIDTH + 2 * 2 * SCORE_CELLS * DH
@@ -41,10 +41,7 @@ def tile_localselfattention_pa_t_kernel(tc, q, k_scaled, hidden_states, Wv, out)
         const = ctx.enter_context(tc.tile_pool(name="const", bufs=1))
         raw = ctx.enter_context(tc.tile_pool(name="raw", bufs=1))
         work = ctx.enter_context(tc.tile_pool(name="work", bufs=2))
-        score_psum = ctx.enter_context(tc.psum_pool(name="score_psum", bufs=2))
-        flip_psum = ctx.enter_context(tc.psum_pool(name="flip_psum", bufs=2))
-        sum_psum = ctx.enter_context(tc.psum_pool(name="sum_psum", bufs=1))
-        prep_psum = ctx.enter_context(tc.psum_pool(name="prep_psum", bufs=1))
+        psum = ctx.enter_context(tc.psum_pool(name="psum", bufs=8))
 
         q_raw, k_raw, h_raw = {}, {}, {}
         w_raw = raw.tile([P, HID_PASSES * PACK * WIDTH], BF16)
@@ -59,7 +56,8 @@ def tile_localselfattention_pa_t_kernel(tc, q, k_scaled, hidden_states, Wv, out)
                     in_=Wv.rearrange("(s p e) n -> p s (e n)", p=P, e=2),
                 )
             h_raw[c] = raw.tile([P, TILES * HID], BF16, name="h_raw%d" % c)
-            nc.sync.dma_start(out=h_raw[c][:].rearrange("p (t k) -> p t k", t=TILES), in_=h_rows[c])
+            for t in range(TILES):
+                nc.sync.dma_start(out=h_raw[c][:, t * HID:(t + 1) * HID], in_=h_rows[c][:, t, :])
 
         ident_bf = const.tile([P, P], BF16)
         make_identity(nc, ident_bf[:])
@@ -73,8 +71,12 @@ def tile_localselfattention_pa_t_kernel(tc, q, k_scaled, hidden_states, Wv, out)
         )
         mask_bf = const.tile([P, P], BF16)
         nc.vector.tensor_copy(out=mask_bf[:], in_=mask_f32[:])
-        zero_block = const.tile([P, P], BF16)
-        nc.vector.memset(zero_block[:], 0.0)
+        e_grp = {}
+        for i in range(TILES):
+            for h in range(HEADS):
+                e_grp[(i, h)] = const.tile([P, 2 * CHUNK], BF16, align_bytes=64, name="e_grp_%d_%d" % (i, h))
+                if i < TILES - 1:
+                    nc.vector.memset(e_grp[(i, h)][:, :CHUNK], 0.0)
 
         w_grp = const.tile([P, HID_PASSES * WIDTH * PACK], BF16, align_bytes=64)
         w_codes = const.tile([P, HID_PASSES * WIDTH], U32, align_bytes=64)
@@ -91,21 +93,21 @@ def tile_localselfattention_pa_t_kernel(tc, q, k_scaled, hidden_states, Wv, out)
         def prepare_on_tensor(c, piece):
             if piece < 2:
                 src = k_raw[c] if piece == 0 else q_raw[c]
-                bank = prep_psum.tile([P, HEADS, TILES, P], BF16, tag="prep", name="qk_bank")
+                bank = psum.tile([P, HEADS, TILES, P], BF16, tag="bank", name="qk_bank")
                 for h in range(HEADS):
                     for i in range(TILES):
                         nc.tensor.transpose(bank[:, h, i, :], src[:, i, h * DH:(h + 1) * DH], ident_bf[:])
             elif piece < 2 + TILES:
                 t = piece - 2
                 words = h_raw[c][:].bitcast(F32)
-                bank = prep_psum.tile([P, HID_PASSES, 2, P], F32, tag="prep", name="h_bank")
+                bank = psum.tile([P, HID_PASSES, 2, P], F32, tag="bank", name="h_bank")
                 for g in range(HID_PASSES):
                     for a in range(2):
                         first = (t * HID_PASSES * 2 + g * 2 + a) * P
                         nc.tensor.transpose(bank[:, g, a, :], words[:, first:first + P], ident_f32[:])
             else:
                 h = piece - 2 - TILES
-                bank = prep_psum.tile([P, TILES, DH], F32, tag="prep", name="v_bank")
+                bank = psum.tile([P, TILES, DH], F32, tag="bank", name="v_bank")
                 for t in range(TILES):
                     for g in range(HID_PASSES):
                         rows = slice((t * HID_PASSES + g) * P, (t * HID_PASSES + g + 1) * P)
@@ -123,10 +125,11 @@ def tile_localselfattention_pa_t_kernel(tc, q, k_scaled, hidden_states, Wv, out)
             if piece < 2:
                 flipped = work.tile([P, HEADS, CHUNK], BF16, tag="k_t" if piece == 0 else "q_t",
                                     bufs=3 if piece == 0 else 2, name="flipped")
-                nc.vector.tensor_copy(out=flipped[:], in_=bank[:].rearrange("p h i x -> p h (i x)"))
                 if piece == 0:
+                    nc.vector.tensor_copy(out=flipped[:], in_=bank[:].rearrange("p h i x -> p h (i x)"))
                     k_t[c] = flipped
                 else:
+                    nc.scalar.copy(out=flipped[:], in_=bank[:].rearrange("p h i x -> p h (i x)"))
                     q_t[c] = flipped
             elif piece < 2 + TILES:
                 t = piece - 2
@@ -136,7 +139,7 @@ def tile_localselfattention_pa_t_kernel(tc, q, k_scaled, hidden_states, Wv, out)
                     h_scales[c] = work.tile([P, TILES * HID_PASSES * P], U8, align_bytes=64, name="h_scales")
                 grouped = h_grp[c][:].bitcast(F32).rearrange(
                     "p (t g x a) -> p t g x a", t=TILES, g=HID_PASSES, a=2)
-                nc.vector.tensor_copy(out=grouped[:, t], in_=bank[:].rearrange("p g a x -> p g x a"))
+                nc.scalar.copy(out=grouped[:, t], in_=bank[:].rearrange("p g a x -> p g x a"))
                 words = slice(t * HID_PASSES * P, (t + 1) * HID_PASSES * P)
                 nc.vector.quantize_mx(
                     out=h_codes[c][:, words].bitcast(FP8X4), scales=h_scales[c][:, words],
@@ -148,7 +151,7 @@ def tile_localselfattention_pa_t_kernel(tc, q, k_scaled, hidden_states, Wv, out)
                     v_grp[c] = work.tile([P, WIDTH * PACK], BF16, align_bytes=64, name="v_grp")
                     v_codes[c] = work.tile([P, WIDTH], U32, align_bytes=64, bufs=3, name="v_codes")
                     v_scales[c] = work.tile([P, WIDTH], U8, align_bytes=64, bufs=3, name="v_scales")
-                nc.vector.tensor_copy(
+                nc.scalar.copy(
                     out=v_grp[c][:, h * DH * PACK:(h + 1) * DH * PACK].rearrange("p (d t) -> p d t", t=PACK),
                     in_=bank[:].rearrange("p t d -> p d t"),
                 )
@@ -156,21 +159,21 @@ def tile_localselfattention_pa_t_kernel(tc, q, k_scaled, hidden_states, Wv, out)
                     nc.vector.quantize_mx(out=v_codes[c][:].bitcast(FP8X4), scales=v_scales[c][:], in_=v_grp[c][:])
 
         units = [(c, i, h) for c in range(N_CHUNKS) for i in range(TILES) for h in range(HEADS)]
-        s_own, s_prev, neg_max, e_rows, e_bank, e_grp, e_codes, e_scales = {}, {}, {}, {}, {}, {}, {}, {}
+        s_own, s_prev, neg_max, e_rows, e_bank, e_codes, e_scales = {}, {}, {}, {}, {}, {}, {}
         row_sums, inverse, acc = {}, {}, {}
 
         def scores_own(u):
             c, i, h = units[u]
             seen = (i + 1) * P
             queries = q_t[c][:, h, i * P:(i + 1) * P]
-            s_own[u] = score_psum.tile([P, CHUNK], F32, name="s_own")
+            s_own[u] = psum.tile([P, CHUNK], F32, tag="bank", name="s_own")
             nc.tensor.matmul(s_own[u][:, :seen], lhsT=queries, rhs=k_t[c][:, h, :seen], start=True, stop=False)
             nc.tensor.matmul(s_own[u][:, i * P:seen], lhsT=ident_bf[:], rhs=mask_bf[:], start=False, stop=True)
 
         def scores_prev(u):
             c, i, h = units[u]
             if c > 0:
-                s_prev[u] = score_psum.tile([P, CHUNK], F32, name="s_prev")
+                s_prev[u] = psum.tile([P, CHUNK], F32, tag="bank", name="s_prev")
                 nc.tensor.matmul(s_prev[u][:], lhsT=q_t[c][:, h, i * P:(i + 1) * P], rhs=k_t[c - 1][:, h, :],
                                  start=True, stop=True)
 
@@ -201,22 +204,24 @@ def tile_localselfattention_pa_t_kernel(tc, q, k_scaled, hidden_states, Wv, out)
 
         def flip(u):
             c, i, h = units[u]
-            e_bank[u] = flip_psum.tile([P, 2, PACK, P], BF16, name="e_bank")
-            for t in range(PACK):
-                block = e_rows[u][:, t * P:(t + 1) * P] if t <= i else zero_block[:]
-                nc.tensor.transpose(e_bank[u][:, 0, t, :], block, ident_bf[:])
+            e_bank[u] = psum.tile([P, 2, PACK, P], BF16, tag="bank", name="e_bank")
+            for t in range(i + 1):
+                nc.tensor.transpose(e_bank[u][:, 0, t, :], e_rows[u][:, t * P:(t + 1) * P], ident_bf[:])
             if c > 0:
                 for t in range(PACK):
                     nc.tensor.transpose(e_bank[u][:, 1, t, :], e_rows[u][:, CHUNK + t * P:CHUNK + (t + 1) * P], ident_bf[:])
 
         def regroup(u):
             c, i, h = units[u]
-            sides = 1 if c == 0 else 2
-            e_grp[u] = work.tile([P, 2 * CHUNK], BF16, align_bytes=64, bufs=3, name="e_grp")
-            nc.scalar.copy(
-                out=e_grp[u][:, :sides * CHUNK].rearrange("p (s x t) -> p s x t", s=sides, t=PACK),
-                in_=e_bank[u][:, :sides].rearrange("p s t x -> p s x t"),
+            nc.vector.tensor_copy(
+                out=e_grp[(i, h)][:, :CHUNK].rearrange("p (x t) -> p x t", t=PACK)[:, :, :i + 1],
+                in_=e_bank[u][:, 0, :i + 1, :].rearrange("p t x -> p x t"),
             )
+            if c > 0:
+                nc.scalar.copy(
+                    out=e_grp[(i, h)][:, CHUNK:].rearrange("p (x t) -> p x t", t=PACK),
+                    in_=e_bank[u][:, 1].rearrange("p t x -> p x t"),
+                )
 
         def quantise(u):
             c, i, h = units[u]
@@ -224,12 +229,12 @@ def tile_localselfattention_pa_t_kernel(tc, q, k_scaled, hidden_states, Wv, out)
             e_codes[u] = work.tile([P, 2 * P], U32, align_bytes=64, bufs=3, name="e_codes")
             e_scales[u] = work.tile([P, 2 * P], U8, align_bytes=64, bufs=3, name="e_scales")
             nc.vector.quantize_mx(out=e_codes[u][:, :sides * P].bitcast(FP8X4), scales=e_scales[u][:, :sides * P],
-                                  in_=e_grp[u][:, :sides * CHUNK])
+                                  in_=e_grp[(i, h)][:, :sides * CHUNK])
 
         def weighted_sum(u):
             c, i, h = units[u]
             if h == 0:
-                acc[(c, i)] = sum_psum.tile([P, HEADS, DH], F32, name="acc")
+                acc[(c, i)] = psum.tile([P, HEADS, DH], F32, tag="bank", name="acc")
             cols = slice(h * DH, (h + 1) * DH)
             nc.tensor.matmul_mx(
                 out=acc[(c, i)][:, h, :],
@@ -265,29 +270,27 @@ def tile_localselfattention_pa_t_kernel(tc, q, k_scaled, hidden_states, Wv, out)
         pieces = 2 + TILES + HEADS
         assert pieces == TILES * HEADS
         n = len(units)
-        with tc.manual_schedule():
-            for k in range(-LEAD, n + 3):
-                if 0 <= k - 3 and units[k - 3][2] == HEADS - 1:
-                    finish(units[k - 3][0], units[k - 3][1])
-                if 0 <= k - 2 < n:
-                    quantise(k - 2)
-                if 0 <= k + LEAD - 1 < n:
-                    prepare_on_vector((k + LEAD - 1) // pieces, (k + LEAD - 1) % pieces)
-                if 0 <= k - 2 < n and units[k - 2][2] == HEADS - 1:
-                    invert_sums(units[k - 2][0], units[k - 2][1])
-                if 0 <= k - 1 < n:
-                    flip(k - 1)
-                if 0 <= k < n:
-                    exponentials(k)
-                if 0 <= k + 1 < n:
-                    scores_own(k + 1)
-                if 0 <= k - 1 < n:
-                    regroup(k - 1)
-                if 0 <= k - 2 < n:
-                    weighted_sum(k - 2)
-                if 0 <= k + 1 < n:
-                    scores_prev(k + 1)
-                if 0 <= k + LEAD < n:
-                    prepare_on_tensor((k + LEAD) // pieces, (k + LEAD) % pieces)
-                if 0 <= k + 1 < n:
-                    maxima(k + 1)
+        for k in range(-LEAD, n + 4):
+            if 0 <= k - 4 and units[k - 4][2] == HEADS - 1:
+                finish(units[k - 4][0], units[k - 4][1])
+            if 0 <= k + 1 < n:
+                maxima(k + 1)
+            if 0 <= k < n:
+                exponentials(k)
+            if 0 <= k - 1 < n:
+                flip(k - 1)
+            if 0 <= k - 3 < n:
+                weighted_sum(k - 3)
+            if 0 <= k + LEAD - 1 < n:
+                prepare_on_vector((k + LEAD - 1) // pieces, (k + LEAD - 1) % pieces)
+            if 0 <= k + 2 < n:
+                scores_own(k + 2)
+                scores_prev(k + 2)
+            if 0 <= k - 1 < n:
+                regroup(k - 1)
+            if 0 <= k - 2 < n:
+                quantise(k - 2)
+            if 0 <= k - 2 < n and units[k - 2][2] == HEADS - 1:
+                invert_sums(units[k - 2][0], units[k - 2][1])
+            if 0 <= k + LEAD < n:
+                prepare_on_tensor((k + LEAD) // pieces, (k + LEAD) % pieces)

@@ -159,8 +159,8 @@ def tile_localselfattention_pa_t_kernel(tc, q, k_scaled, hidden_states, Wv, out)
                     nc.vector.quantize_mx(out=v_codes[c][:].bitcast(FP8X4), scales=v_scales[c][:], in_=v_grp[c][:])
 
         units = [(c, i, h) for c in range(N_CHUNKS) for i in range(TILES) for h in range(HEADS)]
-        s_own, s_prev, neg_max, e_rows, e_bank, e_codes, e_scales = {}, {}, {}, {}, {}, {}, {}
-        row_sums, inverse, acc = {}, {}, {}
+        s_own, s_prev, neg_max, e_rows, own_bank, prev_bank, e_codes, e_scales = {}, {}, {}, {}, {}, {}, {}, {}
+        neg_s, neg_max_prev, row_sums, inverse, acc = {}, {}, {}, {}, {}
 
         def scores_own(u):
             c, i, h = units[u]
@@ -177,50 +177,51 @@ def tile_localselfattention_pa_t_kernel(tc, q, k_scaled, hidden_states, Wv, out)
                 nc.tensor.matmul(s_prev[u][:], lhsT=q_t[c][:, h, i * P:(i + 1) * P], rhs=k_t[c - 1][:, h, :],
                                  start=True, stop=True)
 
-        def maxima(u):
+        def leave_psum_prev(u):
+            c, i, h = units[u]
+            neg_s[u] = work.tile([P, 2 * CHUNK], F32, bufs=4, name="neg_s")
+            if c > 0:
+                neg_max_prev[u] = work.tile([P, 1], F32, bufs=4, name="neg_max_prev")
+                nc.vector.tensor_scalar(out=neg_s[u][:, :CHUNK], in0=s_prev[u][:], scalar1=-1.0, scalar2=None,
+                                        op0=ALU.mult, op1=ALU.min, accum_out=neg_max_prev[u][:])
+
+        def leave_psum_own(u):
             c, i, h = units[u]
             seen = (i + 1) * P
             neg_max[u] = work.tile([P, 1], F32, bufs=4, name="neg_max")
-            if c == 0:
-                nc.vector.tensor_reduce(out=neg_max[u][:], in_=s_own[u][:, :seen], axis=AXIS.X, op=ALU.max, negate=True)
-            else:
-                both = work.tile([P, 2], F32, bufs=4, name="both")
-                nc.vector.tensor_reduce(out=both[:, 0:1], in_=s_own[u][:, :seen], axis=AXIS.X, op=ALU.max)
-                nc.vector.tensor_reduce(out=both[:, 1:2], in_=s_prev[u][:], axis=AXIS.X, op=ALU.max)
-                nc.vector.tensor_reduce(out=neg_max[u][:], in_=both[:], axis=AXIS.X, op=ALU.max, negate=True)
+            nc.vector.tensor_scalar(out=neg_s[u][:, CHUNK:CHUNK + seen], in0=s_own[u][:, :seen], scalar1=-1.0,
+                                    scalar2=None if c == 0 else neg_max_prev[u][:],
+                                    op0=ALU.mult, op1=ALU.min, accum_out=neg_max[u][:])
 
         def exponentials(u):
             c, i, h = units[u]
-            seen = (i + 1) * P
             if h == 0:
-                row_sums[(c, i)] = work.tile([P, HEADS, 2], F32, bufs=4, name="row_sums")
-            sums = row_sums[(c, i)]
+                row_sums[(c, i)] = work.tile([P, HEADS], F32, bufs=4, name="row_sums")
+            keys = slice(CHUNK if c == 0 else 0, CHUNK + (i + 1) * P)
             e_rows[u] = work.tile([P, 2 * CHUNK], BF16, bufs=3, name="e_rows")
-            nc.scalar.activation(out=e_rows[u][:, :seen], in_=s_own[u][:, :seen], func=ACT.Exp,
-                                 bias=neg_max[u][:], scale=1.0, accum_out=sums[:, h, 0:1])
-            if c > 0:
-                nc.scalar.activation(out=e_rows[u][:, CHUNK:], in_=s_prev[u][:], func=ACT.Exp,
-                                     bias=neg_max[u][:], scale=1.0, accum_out=sums[:, h, 1:2])
+            nc.scalar.activation(out=e_rows[u][:, keys], in_=neg_s[u][:, keys], func=ACT.Exp,
+                                 bias=neg_max[u][:], scale=-1.0, accum_out=row_sums[(c, i)][:, h:h + 1])
 
         def flip(u):
             c, i, h = units[u]
-            e_bank[u] = psum.tile([P, 2, PACK, P], BF16, tag="bank", name="e_bank")
+            own_bank[u] = psum.tile([P, PACK, P], BF16, tag="bank", name="own_bank")
             for t in range(i + 1):
-                nc.tensor.transpose(e_bank[u][:, 0, t, :], e_rows[u][:, t * P:(t + 1) * P], ident_bf[:])
+                nc.tensor.transpose(own_bank[u][:, t, :], e_rows[u][:, CHUNK + t * P:CHUNK + (t + 1) * P], ident_bf[:])
             if c > 0:
+                prev_bank[u] = psum.tile([P, PACK, P], BF16, tag="bank", name="prev_bank")
                 for t in range(PACK):
-                    nc.tensor.transpose(e_bank[u][:, 1, t, :], e_rows[u][:, CHUNK + t * P:CHUNK + (t + 1) * P], ident_bf[:])
+                    nc.tensor.transpose(prev_bank[u][:, t, :], e_rows[u][:, t * P:(t + 1) * P], ident_bf[:])
 
         def regroup(u):
             c, i, h = units[u]
             nc.vector.tensor_copy(
                 out=e_grp[(i, h)][:, :CHUNK].rearrange("p (x t) -> p x t", t=PACK)[:, :, :i + 1],
-                in_=e_bank[u][:, 0, :i + 1, :].rearrange("p t x -> p x t"),
+                in_=own_bank[u][:, :i + 1, :].rearrange("p t x -> p x t"),
             )
             if c > 0:
                 nc.scalar.copy(
                     out=e_grp[(i, h)][:, CHUNK:].rearrange("p (x t) -> p x t", t=PACK),
-                    in_=e_bank[u][:, 1].rearrange("p t x -> p x t"),
+                    in_=prev_bank[u][:].rearrange("p t x -> p x t"),
                 )
 
         def quantise(u):
@@ -252,12 +253,7 @@ def tile_localselfattention_pa_t_kernel(tc, q, k_scaled, hidden_states, Wv, out)
 
         def invert_sums(c, i):
             inverse[(c, i)] = work.tile([P, HEADS], F32, bufs=4, name="inverse")
-            if c == 0:
-                nc.vector.reciprocal(out=inverse[(c, i)][:], in_=row_sums[(c, i)][:, :, 0])
-            else:
-                total = work.tile([P, HEADS], F32, bufs=4, name="total")
-                nc.vector.tensor_reduce(out=total[:], in_=row_sums[(c, i)][:], axis=AXIS.X, op=ALU.add)
-                nc.vector.reciprocal(out=inverse[(c, i)][:], in_=total[:])
+            nc.vector.reciprocal(out=inverse[(c, i)][:], in_=row_sums[(c, i)][:])
 
         def finish(c, i):
             result = work.tile([P, WIDTH], F32, bufs=4, name="result")
@@ -271,16 +267,21 @@ def tile_localselfattention_pa_t_kernel(tc, q, k_scaled, hidden_states, Wv, out)
         assert pieces == TILES * HEADS
         n = len(units)
         for k in range(-LEAD, n + 4):
+            last_head = 0 <= k - 2 < n and units[k - 2][2] == HEADS - 1
+            if 0 <= k + 1 < n:
+                leave_psum_prev(k + 1)
             if 0 <= k - 4 and units[k - 4][2] == HEADS - 1:
                 finish(units[k - 4][0], units[k - 4][1])
-            if 0 <= k + 1 < n:
-                maxima(k + 1)
             if 0 <= k < n:
                 exponentials(k)
             if 0 <= k - 1 < n:
                 flip(k - 1)
             if 0 <= k - 3 < n:
                 weighted_sum(k - 3)
+            if 0 <= k - 2 < n:
+                quantise(k - 2)
+            if 0 <= k + 1 < n:
+                leave_psum_own(k + 1)
             if 0 <= k + LEAD - 1 < n:
                 prepare_on_vector((k + LEAD - 1) // pieces, (k + LEAD - 1) % pieces)
             if 0 <= k + 2 < n:
@@ -288,9 +289,7 @@ def tile_localselfattention_pa_t_kernel(tc, q, k_scaled, hidden_states, Wv, out)
                 scores_prev(k + 2)
             if 0 <= k - 1 < n:
                 regroup(k - 1)
-            if 0 <= k - 2 < n:
-                quantise(k - 2)
-            if 0 <= k - 2 < n and units[k - 2][2] == HEADS - 1:
+            if last_head:
                 invert_sums(units[k - 2][0], units[k - 2][1])
             if 0 <= k + LEAD < n:
                 prepare_on_tensor((k + LEAD) // pieces, (k + LEAD) % pieces)

@@ -73,10 +73,9 @@ def tile_localselfattention_pa_t_kernel(tc, q, k_scaled, hidden_states, Wv, out)
         nc.vector.tensor_copy(out=mask_bf[:], in_=mask_f32[:])
         e_grp = {}
         for i in range(TILES):
-            for h in range(HEADS):
-                e_grp[(i, h)] = const.tile([P, 2 * CHUNK], BF16, align_bytes=64, name="e_grp_%d_%d" % (i, h))
-                if i < TILES - 1:
-                    nc.vector.memset(e_grp[(i, h)][:, :CHUNK], 0.0)
+            e_grp[i] = const.tile([P, 2 * HEADS * CHUNK], BF16, align_bytes=64, name="e_grp_%d" % i)
+            if i < TILES - 1:
+                nc.vector.memset(e_grp[i][:, :HEADS * CHUNK], 0.0)
 
         w_grp = const.tile([P, HID_PASSES * WIDTH * PACK], BF16, align_bytes=64)
         w_codes = const.tile([P, HID_PASSES * WIDTH], U32, align_bytes=64)
@@ -160,7 +159,7 @@ def tile_localselfattention_pa_t_kernel(tc, q, k_scaled, hidden_states, Wv, out)
 
         units = [(c, i, h) for c in range(N_CHUNKS) for i in range(TILES) for h in range(HEADS)]
         s_own, s_prev, neg_max, e_rows, own_bank, prev_bank, e_codes, e_scales = {}, {}, {}, {}, {}, {}, {}, {}
-        neg_s, neg_max_prev, row_sums, inverse, acc = {}, {}, {}, {}, {}
+        row_sums, inverse, acc = {}, {}, {}
 
         def scores_own(u):
             c, i, h = units[u]
@@ -177,83 +176,86 @@ def tile_localselfattention_pa_t_kernel(tc, q, k_scaled, hidden_states, Wv, out)
                 nc.tensor.matmul(s_prev[u][:], lhsT=q_t[c][:, h, i * P:(i + 1) * P], rhs=k_t[c - 1][:, h, :],
                                  start=True, stop=True)
 
-        def leave_psum_prev(u):
-            c, i, h = units[u]
-            neg_s[u] = work.tile([P, 2 * CHUNK], F32, bufs=4, name="neg_s")
-            if c > 0:
-                neg_max_prev[u] = work.tile([P, 1], F32, bufs=4, name="neg_max_prev")
-                nc.vector.tensor_scalar(out=neg_s[u][:, :CHUNK], in0=s_prev[u][:], scalar1=-1.0, scalar2=None,
-                                        op0=ALU.mult, op1=ALU.min, accum_out=neg_max_prev[u][:])
-
-        def leave_psum_own(u):
+        def maxima(u):
             c, i, h = units[u]
             seen = (i + 1) * P
             neg_max[u] = work.tile([P, 1], F32, bufs=4, name="neg_max")
-            nc.vector.tensor_scalar(out=neg_s[u][:, CHUNK:CHUNK + seen], in0=s_own[u][:, :seen], scalar1=-1.0,
-                                    scalar2=None if c == 0 else neg_max_prev[u][:],
-                                    op0=ALU.mult, op1=ALU.min, accum_out=neg_max[u][:])
+            if c == 0:
+                nc.vector.tensor_reduce(out=neg_max[u][:], in_=s_own[u][:, :seen], axis=AXIS.X, op=ALU.max, negate=True)
+            else:
+                both = work.tile([P, 2], F32, bufs=4, name="both")
+                nc.vector.tensor_reduce(out=both[:, 0:1], in_=s_own[u][:, :seen], axis=AXIS.X, op=ALU.max)
+                nc.vector.tensor_reduce(out=both[:, 1:2], in_=s_prev[u][:], axis=AXIS.X, op=ALU.max)
+                nc.vector.tensor_reduce(out=neg_max[u][:], in_=both[:], axis=AXIS.X, op=ALU.max, negate=True)
 
         def exponentials(u):
             c, i, h = units[u]
+            seen = (i + 1) * P
             if h == 0:
-                row_sums[(c, i)] = work.tile([P, HEADS], F32, bufs=4, name="row_sums")
-            keys = slice(CHUNK if c == 0 else 0, CHUNK + (i + 1) * P)
-            e_rows[u] = work.tile([P, 2 * CHUNK], BF16, bufs=3, name="e_rows")
-            nc.scalar.activation(out=e_rows[u][:, keys], in_=neg_s[u][:, keys], func=ACT.Exp,
-                                 bias=neg_max[u][:], scale=-1.0, accum_out=row_sums[(c, i)][:, h:h + 1])
-
-        def flip(u):
-            c, i, h = units[u]
-            own_bank[u] = psum.tile([P, PACK, P], BF16, tag="bank", name="own_bank")
-            for t in range(i + 1):
-                nc.tensor.transpose(own_bank[u][:, t, :], e_rows[u][:, CHUNK + t * P:CHUNK + (t + 1) * P], ident_bf[:])
+                row_sums[(c, i)] = work.tile([P, HEADS, 2], F32, bufs=4, name="row_sums")
+            sums = row_sums[(c, i)]
+            e_rows[u] = work.tile([P, 2 * CHUNK], BF16, bufs=5, name="e_rows")
+            nc.scalar.activation(out=e_rows[u][:, :seen], in_=s_own[u][:, :seen], func=ACT.Exp,
+                                 bias=neg_max[u][:], scale=1.0, accum_out=sums[:, h, 0:1])
             if c > 0:
-                prev_bank[u] = psum.tile([P, PACK, P], BF16, tag="bank", name="prev_bank")
-                for t in range(PACK):
-                    nc.tensor.transpose(prev_bank[u][:, t, :], e_rows[u][:, t * P:(t + 1) * P], ident_bf[:])
+                nc.scalar.activation(out=e_rows[u][:, CHUNK:], in_=s_prev[u][:], func=ACT.Exp,
+                                     bias=neg_max[u][:], scale=1.0, accum_out=sums[:, h, 1:2])
 
-        def regroup(u):
-            c, i, h = units[u]
+        def flip(c, i):
+            own_bank[(c, i)] = psum.tile([P, HEADS, PACK, P], BF16, tag="bank", name="own_bank")
+            for h in range(HEADS):
+                rows = e_rows[(c * TILES + i) * HEADS + h]
+                for t in range(i + 1):
+                    nc.tensor.transpose(own_bank[(c, i)][:, h, t, :], rows[:, t * P:(t + 1) * P], ident_bf[:])
+            if c > 0:
+                prev_bank[(c, i)] = psum.tile([P, HEADS, PACK, P], BF16, tag="bank", name="prev_bank")
+                for h in range(HEADS):
+                    rows = e_rows[(c * TILES + i) * HEADS + h]
+                    for t in range(PACK):
+                        nc.tensor.transpose(prev_bank[(c, i)][:, h, t, :], rows[:, CHUNK + t * P:CHUNK + (t + 1) * P],
+                                            ident_bf[:])
+
+        def regroup(c, i):
             nc.vector.tensor_copy(
-                out=e_grp[(i, h)][:, :CHUNK].rearrange("p (x t) -> p x t", t=PACK)[:, :, :i + 1],
-                in_=own_bank[u][:, :i + 1, :].rearrange("p t x -> p x t"),
+                out=e_grp[i][:, :HEADS * CHUNK].rearrange("p (h x t) -> p h x t", h=HEADS, t=PACK)[:, :, :, :i + 1],
+                in_=own_bank[(c, i)][:, :, :i + 1, :].rearrange("p h t x -> p h x t"),
             )
             if c > 0:
                 nc.scalar.copy(
-                    out=e_grp[(i, h)][:, CHUNK:].rearrange("p (x t) -> p x t", t=PACK),
-                    in_=prev_bank[u][:].rearrange("p t x -> p x t"),
+                    out=e_grp[i][:, HEADS * CHUNK:].rearrange("p (h x t) -> p h x t", h=HEADS, t=PACK),
+                    in_=prev_bank[(c, i)][:].rearrange("p h t x -> p h x t"),
                 )
 
-        def quantise(u):
-            c, i, h = units[u]
+        def quantise(c, i):
             sides = 1 if c == 0 else 2
-            e_codes[u] = work.tile([P, 2 * P], U32, align_bytes=64, bufs=3, name="e_codes")
-            e_scales[u] = work.tile([P, 2 * P], U8, align_bytes=64, bufs=3, name="e_scales")
-            nc.vector.quantize_mx(out=e_codes[u][:, :sides * P].bitcast(FP8X4), scales=e_scales[u][:, :sides * P],
-                                  in_=e_grp[(i, h)][:, :sides * CHUNK])
-
-        def weighted_sum(u):
-            c, i, h = units[u]
-            if h == 0:
-                acc[(c, i)] = psum.tile([P, HEADS, DH], F32, tag="bank", name="acc")
-            cols = slice(h * DH, (h + 1) * DH)
-            nc.tensor.matmul_mx(
-                out=acc[(c, i)][:, h, :],
-                lhsT=e_codes[u][:, :P].bitcast(FP8X4), lhsT_scale=e_scales[u][:, :P],
-                rhs=v_codes[c][:, cols].bitcast(FP8X4), rhs_scale=v_scales[c][:, cols],
-                start=True, stop=(c == 0),
+            e_codes[(c, i)] = work.tile([P, 2 * HEADS * P], U32, align_bytes=64, bufs=3, name="e_codes")
+            e_scales[(c, i)] = work.tile([P, 2 * HEADS * P], U8, align_bytes=64, bufs=3, name="e_scales")
+            nc.vector.quantize_mx(
+                out=e_codes[(c, i)][:, :sides * HEADS * P].bitcast(FP8X4), scales=e_scales[(c, i)][:, :sides * HEADS * P],
+                in_=e_grp[i][:, :sides * HEADS * CHUNK],
             )
-            if c > 0:
-                nc.tensor.matmul_mx(
-                    out=acc[(c, i)][:, h, :],
-                    lhsT=e_codes[u][:, P:].bitcast(FP8X4), lhsT_scale=e_scales[u][:, P:],
-                    rhs=v_codes[c - 1][:, cols].bitcast(FP8X4), rhs_scale=v_scales[c - 1][:, cols],
-                    start=False, stop=True,
-                )
+
+        def weighted_sum(c, i):
+            acc[(c, i)] = psum.tile([P, HEADS, DH], F32, tag="bank", name="acc")
+            for h in range(HEADS):
+                for side in range(1 if c == 0 else 2):
+                    queries = slice((side * HEADS + h) * P, (side * HEADS + h + 1) * P)
+                    features = slice(h * DH, (h + 1) * DH)
+                    nc.tensor.matmul_mx(
+                        out=acc[(c, i)][:, h, :],
+                        lhsT=e_codes[(c, i)][:, queries].bitcast(FP8X4), lhsT_scale=e_scales[(c, i)][:, queries],
+                        rhs=v_codes[c - side][:, features].bitcast(FP8X4), rhs_scale=v_scales[c - side][:, features],
+                        start=(side == 0), stop=(side == 1 or c == 0),
+                    )
 
         def invert_sums(c, i):
             inverse[(c, i)] = work.tile([P, HEADS], F32, bufs=4, name="inverse")
-            nc.vector.reciprocal(out=inverse[(c, i)][:], in_=row_sums[(c, i)][:])
+            if c == 0:
+                nc.vector.reciprocal(out=inverse[(c, i)][:], in_=row_sums[(c, i)][:, :, 0])
+            else:
+                total = work.tile([P, HEADS], F32, bufs=4, name="total")
+                nc.vector.tensor_reduce(out=total[:], in_=row_sums[(c, i)][:], axis=AXIS.X, op=ALU.add)
+                nc.vector.reciprocal(out=inverse[(c, i)][:], in_=total[:])
 
         def finish(c, i):
             result = work.tile([P, WIDTH], F32, bufs=4, name="result")
@@ -267,29 +269,25 @@ def tile_localselfattention_pa_t_kernel(tc, q, k_scaled, hidden_states, Wv, out)
         assert pieces == TILES * HEADS
         n = len(units)
         for k in range(-LEAD, n + 4):
-            last_head = 0 <= k - 2 < n and units[k - 2][2] == HEADS - 1
-            if 0 <= k + 1 < n:
-                leave_psum_prev(k + 1)
             if 0 <= k - 4 and units[k - 4][2] == HEADS - 1:
                 finish(units[k - 4][0], units[k - 4][1])
+            if 0 <= k + 1 < n:
+                maxima(k + 1)
             if 0 <= k < n:
                 exponentials(k)
-            if 0 <= k - 1 < n:
-                flip(k - 1)
-            if 0 <= k - 3 < n:
-                weighted_sum(k - 3)
-            if 0 <= k - 2 < n:
-                quantise(k - 2)
-            if 0 <= k + 1 < n:
-                leave_psum_own(k + 1)
+            if 0 <= k - 1 < n and units[k - 1][2] == HEADS - 1:
+                flip(units[k - 1][0], units[k - 1][1])
+            if 0 <= k - 3 < n and units[k - 3][2] == HEADS - 1:
+                weighted_sum(units[k - 3][0], units[k - 3][1])
             if 0 <= k + LEAD - 1 < n:
                 prepare_on_vector((k + LEAD - 1) // pieces, (k + LEAD - 1) % pieces)
             if 0 <= k + 2 < n:
                 scores_own(k + 2)
                 scores_prev(k + 2)
-            if 0 <= k - 1 < n:
-                regroup(k - 1)
-            if last_head:
+            if 0 <= k - 1 < n and units[k - 1][2] == HEADS - 1:
+                regroup(units[k - 1][0], units[k - 1][1])
+            if 0 <= k - 2 < n and units[k - 2][2] == HEADS - 1:
+                quantise(units[k - 2][0], units[k - 2][1])
                 invert_sums(units[k - 2][0], units[k - 2][1])
             if 0 <= k + LEAD < n:
                 prepare_on_tensor((k + LEAD) // pieces, (k + LEAD) % pieces)

@@ -34,7 +34,7 @@ def tile_localselfattention_pa_t_kernel(tc, q, k_scaled, hidden_states, Wv, out)
     nc = tc.nc
     q_rows = q.flatten_outer_dims().rearrange("(c i p) w -> c p i w", i=TILES, p=P)
     k_rows = k_scaled.flatten_outer_dims().rearrange("(c i p) w -> c p i w", i=TILES, p=P)
-    h_rows = hidden_states.flatten_outer_dims().rearrange("(c t p) k -> c p t k", t=TILES, p=P)
+    h_rows = hidden_states.flatten_outer_dims().rearrange("(c u p e) k -> c p u (e k)", u=TILES // 2, p=P, e=2)
     out_rows = out.flatten_outer_dims().rearrange("(n p) w -> n p w", p=P)
 
     with ExitStack() as ctx:
@@ -56,8 +56,8 @@ def tile_localselfattention_pa_t_kernel(tc, q, k_scaled, hidden_states, Wv, out)
                     in_=Wv.rearrange("(s p e) n -> p s (e n)", p=P, e=2),
                 )
             h_raw[c] = raw.tile([P, TILES * HID], BF16, name="h_raw%d" % c)
-            for t in range(TILES):
-                nc.sync.dma_start(out=h_raw[c][:, t * HID:(t + 1) * HID], in_=h_rows[c][:, t, :])
+            for u in range(TILES // 2):
+                nc.sync.dma_start(out=h_raw[c][:, 2 * u * HID:2 * (u + 1) * HID], in_=h_rows[c][:, u, :])
 
         ident_bf = const.tile([P, P], BF16)
         make_identity(nc, ident_bf[:])
@@ -71,11 +71,12 @@ def tile_localselfattention_pa_t_kernel(tc, q, k_scaled, hidden_states, Wv, out)
         )
         mask_bf = const.tile([P, P], BF16)
         nc.vector.tensor_copy(out=mask_bf[:], in_=mask_f32[:])
-        e_grp = {}
+        e_rows = {}
         for i in range(TILES):
-            e_grp[i] = const.tile([P, 2 * HEADS * CHUNK], BF16, align_bytes=64, name="e_grp_%d" % i)
-            if i < TILES - 1:
-                nc.vector.memset(e_grp[i][:, :HEADS * CHUNK], 0.0)
+            for h in range(HEADS):
+                e_rows[(i, h)] = const.tile([P, 2 * CHUNK], BF16, align_bytes=64, name="e_rows_%d_%d" % (i, h))
+                if i < TILES - 1:
+                    nc.vector.memset(e_rows[(i, h)][:, (i + 1) * P:CHUNK], 0.0)
 
         w_grp = const.tile([P, HID_PASSES * WIDTH * PACK], BF16, align_bytes=64)
         w_codes = const.tile([P, HID_PASSES * WIDTH], U32, align_bytes=64)
@@ -158,7 +159,7 @@ def tile_localselfattention_pa_t_kernel(tc, q, k_scaled, hidden_states, Wv, out)
                     nc.vector.quantize_mx(out=v_codes[c][:].bitcast(FP8X4), scales=v_scales[c][:], in_=v_grp[c][:])
 
         units = [(c, i, h) for c in range(N_CHUNKS) for i in range(TILES) for h in range(HEADS)]
-        s_own, s_prev, neg_max, e_rows, own_bank, prev_bank, e_codes, e_scales = {}, {}, {}, {}, {}, {}, {}, {}
+        s_own, s_prev, neg_max, own_bank, prev_bank, e_grp, e_codes, e_scales = {}, {}, {}, {}, {}, {}, {}, {}
         row_sums, inverse, acc = {}, {}, {}
 
         def scores_own(u):
@@ -194,37 +195,29 @@ def tile_localselfattention_pa_t_kernel(tc, q, k_scaled, hidden_states, Wv, out)
             if h == 0:
                 row_sums[(c, i)] = work.tile([P, HEADS, 2], F32, bufs=4, name="row_sums")
             sums = row_sums[(c, i)]
-            e_rows[u] = work.tile([P, 2 * CHUNK], BF16, bufs=5, name="e_rows")
-            nc.scalar.activation(out=e_rows[u][:, :seen], in_=s_own[u][:, :seen], func=ACT.Exp,
+            nc.scalar.activation(out=e_rows[(i, h)][:, :seen], in_=s_own[u][:, :seen], func=ACT.Exp,
                                  bias=neg_max[u][:], scale=1.0, accum_out=sums[:, h, 0:1])
             if c > 0:
-                nc.scalar.activation(out=e_rows[u][:, CHUNK:], in_=s_prev[u][:], func=ACT.Exp,
+                nc.scalar.activation(out=e_rows[(i, h)][:, CHUNK:], in_=s_prev[u][:], func=ACT.Exp,
                                      bias=neg_max[u][:], scale=1.0, accum_out=sums[:, h, 1:2])
 
         def flip(c, i):
-            own_bank[(c, i)] = psum.tile([P, HEADS, PACK, P], BF16, tag="bank", name="own_bank")
-            for h in range(HEADS):
-                rows = e_rows[(c * TILES + i) * HEADS + h]
-                for t in range(i + 1):
-                    nc.tensor.transpose(own_bank[(c, i)][:, h, t, :], rows[:, t * P:(t + 1) * P], ident_bf[:])
-            if c > 0:
-                prev_bank[(c, i)] = psum.tile([P, HEADS, PACK, P], BF16, tag="bank", name="prev_bank")
+            for side, banks in ((0, own_bank), (1, prev_bank)):
+                if side == 1 and c == 0:
+                    continue
+                banks[(c, i)] = psum.tile([P, HEADS, 2, P], F32, tag="bank", name="flip_bank")
                 for h in range(HEADS):
-                    rows = e_rows[(c * TILES + i) * HEADS + h]
-                    for t in range(PACK):
-                        nc.tensor.transpose(prev_bank[(c, i)][:, h, t, :], rows[:, CHUNK + t * P:CHUNK + (t + 1) * P],
-                                            ident_bf[:])
+                    words = e_rows[(i, h)][:].bitcast(F32)
+                    for u in range(2):
+                        first = (side * 2 + u) * P
+                        nc.tensor.transpose(banks[(c, i)][:, h, u, :], words[:, first:first + P], ident_f32[:])
 
         def regroup(c, i):
-            nc.vector.tensor_copy(
-                out=e_grp[i][:, :HEADS * CHUNK].rearrange("p (h x t) -> p h x t", h=HEADS, t=PACK)[:, :, :, :i + 1],
-                in_=own_bank[(c, i)][:, :, :i + 1, :].rearrange("p h t x -> p h x t"),
-            )
+            e_grp[(c, i)] = work.tile([P, 2 * HEADS * CHUNK], BF16, align_bytes=64, bufs=3, name="e_grp")
+            grouped = e_grp[(c, i)][:].bitcast(F32).rearrange("p (s h x u) -> p s h x u", s=2, h=HEADS, u=2)
+            nc.vector.tensor_copy(out=grouped[:, 0], in_=own_bank[(c, i)][:].rearrange("p h u x -> p h x u"))
             if c > 0:
-                nc.scalar.copy(
-                    out=e_grp[i][:, HEADS * CHUNK:].rearrange("p (h x t) -> p h x t", h=HEADS, t=PACK),
-                    in_=prev_bank[(c, i)][:].rearrange("p h t x -> p h x t"),
-                )
+                nc.scalar.copy(out=grouped[:, 1], in_=prev_bank[(c, i)][:].rearrange("p h u x -> p h x u"))
 
         def quantise(c, i):
             sides = 1 if c == 0 else 2
@@ -232,7 +225,7 @@ def tile_localselfattention_pa_t_kernel(tc, q, k_scaled, hidden_states, Wv, out)
             e_scales[(c, i)] = work.tile([P, 2 * HEADS * P], U8, align_bytes=64, bufs=3, name="e_scales")
             nc.vector.quantize_mx(
                 out=e_codes[(c, i)][:, :sides * HEADS * P].bitcast(FP8X4), scales=e_scales[(c, i)][:, :sides * HEADS * P],
-                in_=e_grp[i][:, :sides * HEADS * CHUNK],
+                in_=e_grp[(c, i)][:, :sides * HEADS * CHUNK],
             )
 
         def weighted_sum(c, i):

@@ -24,6 +24,7 @@ N_CHUNKS = SEQ // CHUNK
 TILES = CHUNK // P
 HID_PASSES = HID // CHUNK
 MASKED = -1.0e9
+LOWEST = -3.0e38
 LEAD = 6
 
 SCORE_CELLS = HEADS * (2 * N_CHUNKS - 1) * CHUNK * CHUNK
@@ -35,13 +36,14 @@ def tile_localselfattention_pa_t_kernel(tc, q, k_scaled, hidden_states, Wv, out)
     q_rows = q.flatten_outer_dims().rearrange("(c i p) w -> c p i w", i=TILES, p=P)
     k_rows = k_scaled.flatten_outer_dims().rearrange("(c i p) w -> c p i w", i=TILES, p=P)
     h_rows = hidden_states.flatten_outer_dims().rearrange("(c u p e) k -> c p u (e k)", u=TILES // 2, p=P, e=2)
-    out_rows = out.flatten_outer_dims().rearrange("(n p) w -> n p w", p=P)
+    out_rows = out.flatten_outer_dims().rearrange("(n j p) w -> n p j w", j=2, p=P)
 
     with ExitStack() as ctx:
         const = ctx.enter_context(tc.tile_pool(name="const", bufs=1))
         raw = ctx.enter_context(tc.tile_pool(name="raw", bufs=1))
         work = ctx.enter_context(tc.tile_pool(name="work", bufs=2))
-        psum = ctx.enter_context(tc.psum_pool(name="psum", bufs=8))
+        psum = ctx.enter_context(tc.psum_pool(name="psum", bufs=7))
+        psum_sum = ctx.enter_context(tc.psum_pool(name="psum_sum", bufs=1))
 
         q_raw, k_raw, h_raw = {}, {}, {}
         w_raw = raw.tile([P, HID_PASSES * PACK * WIDTH], BF16)
@@ -125,11 +127,10 @@ def tile_localselfattention_pa_t_kernel(tc, q, k_scaled, hidden_states, Wv, out)
             if piece < 2:
                 flipped = work.tile([P, HEADS, CHUNK], BF16, tag="k_t" if piece == 0 else "q_t",
                                     bufs=3 if piece == 0 else 2, name="flipped")
+                nc.scalar.copy(out=flipped[:], in_=bank[:].rearrange("p h i x -> p h (i x)"))
                 if piece == 0:
-                    nc.vector.tensor_copy(out=flipped[:], in_=bank[:].rearrange("p h i x -> p h (i x)"))
                     k_t[c] = flipped
                 else:
-                    nc.scalar.copy(out=flipped[:], in_=bank[:].rearrange("p h i x -> p h (i x)"))
                     q_t[c] = flipped
             elif piece < 2 + TILES:
                 t = piece - 2
@@ -185,21 +186,22 @@ def tile_localselfattention_pa_t_kernel(tc, q, k_scaled, hidden_states, Wv, out)
                 nc.vector.tensor_reduce(out=neg_max[u][:], in_=s_own[u][:, :seen], axis=AXIS.X, op=ALU.max, negate=True)
             else:
                 both = work.tile([P, 2], F32, bufs=4, name="both")
-                nc.vector.tensor_reduce(out=both[:, 0:1], in_=s_own[u][:, :seen], axis=AXIS.X, op=ALU.max)
-                nc.vector.tensor_reduce(out=both[:, 1:2], in_=s_prev[u][:], axis=AXIS.X, op=ALU.max)
-                nc.vector.tensor_reduce(out=neg_max[u][:], in_=both[:], axis=AXIS.X, op=ALU.max, negate=True)
+                nc.vector.tensor_reduce(out=both[:, 0:1], in_=s_own[u][:, :seen], axis=AXIS.X, op=ALU.max, negate=True)
+                nc.vector.tensor_reduce(out=both[:, 1:2], in_=s_prev[u][:], axis=AXIS.X, op=ALU.max, negate=True)
+                nc.gpsimd.tensor_scalar(out=neg_max[u][:], in0=both[:, 0:1], scalar1=both[:, 1:2], scalar2=LOWEST,
+                                        op0=ALU.min, op1=ALU.max)
 
         def exponentials(u):
             c, i, h = units[u]
             seen = (i + 1) * P
-            if h == 0:
-                row_sums[(c, i)] = work.tile([P, HEADS, 2], F32, bufs=4, name="row_sums")
-            sums = row_sums[(c, i)]
+            if i % 2 == 0 and h == 0:
+                row_sums[(c, i // 2)] = work.tile([P, 2, HEADS, 2], F32, bufs=3, name="row_sums")
+            sums = row_sums[(c, i // 2)]
             nc.scalar.activation(out=e_rows[(i, h)][:, :seen], in_=s_own[u][:, :seen], func=ACT.Exp,
-                                 bias=neg_max[u][:], scale=1.0, accum_out=sums[:, h, 0:1])
+                                 bias=neg_max[u][:], scale=1.0, accum_out=sums[:, i % 2, h, 0:1])
             if c > 0:
                 nc.scalar.activation(out=e_rows[(i, h)][:, CHUNK:], in_=s_prev[u][:], func=ACT.Exp,
-                                     bias=neg_max[u][:], scale=1.0, accum_out=sums[:, h, 1:2])
+                                     bias=neg_max[u][:], scale=1.0, accum_out=sums[:, i % 2, h, 1:2])
 
         def flip(c, i):
             for side, banks in ((0, own_bank), (1, prev_bank)):
@@ -229,41 +231,46 @@ def tile_localselfattention_pa_t_kernel(tc, q, k_scaled, hidden_states, Wv, out)
             )
 
         def weighted_sum(c, i):
-            acc[(c, i)] = psum.tile([P, HEADS, DH], F32, tag="bank", name="acc")
+            if i % 2 == 0:
+                acc[(c, i // 2)] = psum_sum.tile([P, 2, HEADS, DH], F32, name="acc")
             for h in range(HEADS):
                 for side in range(1 if c == 0 else 2):
                     queries = slice((side * HEADS + h) * P, (side * HEADS + h + 1) * P)
                     features = slice(h * DH, (h + 1) * DH)
                     nc.tensor.matmul_mx(
-                        out=acc[(c, i)][:, h, :],
+                        out=acc[(c, i // 2)][:, i % 2, h, :],
                         lhsT=e_codes[(c, i)][:, queries].bitcast(FP8X4), lhsT_scale=e_scales[(c, i)][:, queries],
                         rhs=v_codes[c - side][:, features].bitcast(FP8X4), rhs_scale=v_scales[c - side][:, features],
                         start=(side == 0), stop=(side == 1 or c == 0),
                     )
 
-        def invert_sums(c, i):
-            inverse[(c, i)] = work.tile([P, HEADS], F32, bufs=4, name="inverse")
+        def invert_sums(c, j):
+            inverse[(c, j)] = work.tile([P, 2 * HEADS], F32, bufs=3, name="inverse")
+            sums = row_sums[(c, j)][:].rearrange("p t h s -> p (t h) s")
             if c == 0:
-                nc.vector.reciprocal(out=inverse[(c, i)][:], in_=row_sums[(c, i)][:, :, 0])
+                nc.vector.reciprocal(out=inverse[(c, j)][:], in_=sums[:, :, 0])
             else:
-                total = work.tile([P, HEADS], F32, bufs=4, name="total")
-                nc.vector.tensor_reduce(out=total[:], in_=row_sums[(c, i)][:], axis=AXIS.X, op=ALU.add)
-                nc.vector.reciprocal(out=inverse[(c, i)][:], in_=total[:])
+                total = work.tile([P, 2 * HEADS], F32, bufs=3, name="total")
+                nc.vector.tensor_reduce(out=total[:], in_=sums, axis=AXIS.X, op=ALU.add)
+                nc.vector.reciprocal(out=inverse[(c, j)][:], in_=total[:])
 
-        def finish(c, i):
-            result = work.tile([P, WIDTH], F32, bufs=4, name="result")
-            nc.vector.tensor_scalar(out=result[:, :DH], in0=acc[(c, i)][:, 0, :], scalar1=inverse[(c, i)][:, 0:1],
-                                    scalar2=None, op0=ALU.mult)
-            nc.scalar.activation(out=result[:, DH:], in_=acc[(c, i)][:, 1, :], func=ACT.Copy,
-                                 scale=inverse[(c, i)][:, 1:2])
-            nc.sync.dma_start(out=out_rows[c * TILES + i], in_=result[:])
+        def finish(c, j):
+            result = work.tile([P, 2, WIDTH], F32, bufs=3, name="result")
+            nc.vector.tensor_tensor(
+                out=result[:].rearrange("p t (h d) -> p (t h) d", h=HEADS),
+                in0=acc[(c, j)][:].rearrange("p t h d -> p (t h) d"),
+                in1=inverse[(c, j)][:].unsqueeze(2).to_broadcast([P, 2 * HEADS, DH]), op=ALU.mult,
+            )
+            nc.sync.dma_start(out=out_rows[c * TILES // 2 + j], in_=result[:])
 
         pieces = 2 + TILES + HEADS
         assert pieces == TILES * HEADS
         n = len(units)
         for k in range(-LEAD, n + 4):
             if 0 <= k - 4 and units[k - 4][2] == HEADS - 1:
-                finish(units[k - 4][0], units[k - 4][1])
+                c, i, h = units[k - 4]
+                if i % 2 == 1:
+                    finish(c, i // 2)
             if 0 <= k + 1 < n:
                 maxima(k + 1)
             if 0 <= k < n:
@@ -281,6 +288,8 @@ def tile_localselfattention_pa_t_kernel(tc, q, k_scaled, hidden_states, Wv, out)
                 regroup(units[k - 1][0], units[k - 1][1])
             if 0 <= k - 2 < n and units[k - 2][2] == HEADS - 1:
                 quantise(units[k - 2][0], units[k - 2][1])
-                invert_sums(units[k - 2][0], units[k - 2][1])
+                c, i, h = units[k - 2]
+                if i % 2 == 1:
+                    invert_sums(c, i // 2)
             if 0 <= k + LEAD < n:
                 prepare_on_tensor((k + LEAD) // pieces, (k + LEAD) % pieces)

@@ -24,7 +24,6 @@ N_CHUNKS = SEQ // CHUNK
 TILES = CHUNK // P
 HID_PASSES = HID // CHUNK
 MASKED = -1.0e9
-LOWEST = -3.0e38
 LEAD = 6
 
 SCORE_CELLS = HEADS * (2 * N_CHUNKS - 1) * CHUNK * CHUNK
@@ -78,7 +77,7 @@ def tile_localselfattention_pa_t_kernel(tc, q, k_scaled, hidden_states, Wv, out)
             for h in range(HEADS):
                 e_rows[(i, h)] = const.tile([P, 2 * CHUNK], BF16, align_bytes=64, name="e_rows_%d_%d" % (i, h))
                 if i < TILES - 1:
-                    nc.vector.memset(e_rows[(i, h)][:, (i + 1) * P:CHUNK], 0.0)
+                    nc.vector.memset(e_rows[(i, h)][:, CHUNK + (i + 1) * P:], 0.0)
 
         w_grp = const.tile([P, HID_PASSES * WIDTH * PACK], BF16, align_bytes=64)
         w_codes = const.tile([P, HID_PASSES * WIDTH], U32, align_bytes=64)
@@ -160,7 +159,7 @@ def tile_localselfattention_pa_t_kernel(tc, q, k_scaled, hidden_states, Wv, out)
                     nc.vector.quantize_mx(out=v_codes[c][:].bitcast(FP8X4), scales=v_scales[c][:], in_=v_grp[c][:])
 
         units = [(c, i, h) for c in range(N_CHUNKS) for i in range(TILES) for h in range(HEADS)]
-        s_own, s_prev, neg_max, own_bank, prev_bank, e_grp, e_codes, e_scales = {}, {}, {}, {}, {}, {}, {}, {}
+        s_own, s_prev, neg_scores, neg_max, own_bank, prev_bank, e_grp, e_codes, e_scales = {}, {}, {}, {}, {}, {}, {}, {}, {}
         row_sums, inverse, acc = {}, {}, {}
 
         def scores_own(u):
@@ -178,30 +177,29 @@ def tile_localselfattention_pa_t_kernel(tc, q, k_scaled, hidden_states, Wv, out)
                 nc.tensor.matmul(s_prev[u][:], lhsT=q_t[c][:, h, i * P:(i + 1) * P], rhs=k_t[c - 1][:, h, :],
                                  start=True, stop=True)
 
-        def maxima(u):
+        def move_prev(u):
+            neg_scores[u] = work.tile([P, 2 * CHUNK], F32, bufs=4, name="neg_scores")
+            neg_max[u] = work.tile([P, 2], F32, bufs=4, name="neg_max")
+            if units[u][0] > 0:
+                nc.vector.tensor_scalar(out=neg_scores[u][:, :CHUNK], in0=s_prev[u][:], scalar1=-1.0, scalar2=None,
+                                        op0=ALU.mult, op1=ALU.min, accum_out=neg_max[u][:, 0:1])
+
+        def move_own(u):
             c, i, h = units[u]
             seen = (i + 1) * P
-            neg_max[u] = work.tile([P, 1], F32, bufs=4, name="neg_max")
-            if c == 0:
-                nc.vector.tensor_reduce(out=neg_max[u][:], in_=s_own[u][:, :seen], axis=AXIS.X, op=ALU.max, negate=True)
-            else:
-                both = work.tile([P, 2], F32, bufs=4, name="both")
-                nc.vector.tensor_reduce(out=both[:, 0:1], in_=s_own[u][:, :seen], axis=AXIS.X, op=ALU.max, negate=True)
-                nc.vector.tensor_reduce(out=both[:, 1:2], in_=s_prev[u][:], axis=AXIS.X, op=ALU.max, negate=True)
-                nc.gpsimd.tensor_scalar(out=neg_max[u][:], in0=both[:, 0:1], scalar1=both[:, 1:2], scalar2=LOWEST,
-                                        op0=ALU.min, op1=ALU.max)
+            nc.vector.tensor_scalar(out=neg_scores[u][:, CHUNK:CHUNK + seen], in0=s_own[u][:, :seen], scalar1=-1.0,
+                                    scalar2=neg_max[u][:, 0:1] if c > 0 else None,
+                                    op0=ALU.mult, op1=ALU.min, accum_out=neg_max[u][:, 1:2])
 
         def exponentials(u):
             c, i, h = units[u]
-            seen = (i + 1) * P
             if i % 2 == 0 and h == 0:
-                row_sums[(c, i // 2)] = work.tile([P, 2, HEADS, 2], F32, bufs=3, name="row_sums")
-            sums = row_sums[(c, i // 2)]
-            nc.scalar.activation(out=e_rows[(i, h)][:, :seen], in_=s_own[u][:, :seen], func=ACT.Exp,
-                                 bias=neg_max[u][:], scale=1.0, accum_out=sums[:, i % 2, h, 0:1])
-            if c > 0:
-                nc.scalar.activation(out=e_rows[(i, h)][:, CHUNK:], in_=s_prev[u][:], func=ACT.Exp,
-                                     bias=neg_max[u][:], scale=1.0, accum_out=sums[:, i % 2, h, 1:2])
+                row_sums[(c, i // 2)] = work.tile([P, 2 * HEADS], F32, bufs=3, name="row_sums")
+            keys = slice(CHUNK if c == 0 else 0, CHUNK + (i + 1) * P)
+            column = (i % 2) * HEADS + h
+            nc.scalar.activation(out=e_rows[(i, h)][:, keys], in_=neg_scores[u][:, keys], func=ACT.Exp,
+                                 bias=neg_max[u][:, 1:2], scale=-1.0,
+                                 accum_out=row_sums[(c, i // 2)][:, column:column + 1])
 
         def flip(c, i):
             for side, banks in ((0, own_bank), (1, prev_bank)):
@@ -211,13 +209,17 @@ def tile_localselfattention_pa_t_kernel(tc, q, k_scaled, hidden_states, Wv, out)
                 for h in range(HEADS):
                     words = e_rows[(i, h)][:].bitcast(F32)
                     for u in range(2):
-                        first = (side * 2 + u) * P
+                        first = ((1 - side) * 2 + u) * P
                         nc.tensor.transpose(banks[(c, i)][:, h, u, :], words[:, first:first + P], ident_f32[:])
 
         def regroup(c, i):
             e_grp[(c, i)] = work.tile([P, 2 * HEADS * CHUNK], BF16, align_bytes=64, bufs=3, name="e_grp")
             grouped = e_grp[(c, i)][:].bitcast(F32).rearrange("p (s h x u) -> p s h x u", s=2, h=HEADS, u=2)
-            nc.vector.tensor_copy(out=grouped[:, 0], in_=own_bank[(c, i)][:].rearrange("p h u x -> p h x u"))
+            own_words = own_bank[(c, i)][:].rearrange("p h u x -> p h x u")
+            if i % 2 == 0:
+                nc.vector.tensor_copy(out=grouped[:, 0], in_=own_words)
+            else:
+                nc.scalar.copy(out=grouped[:, 0], in_=own_words)
             if c > 0:
                 nc.scalar.copy(out=grouped[:, 1], in_=prev_bank[(c, i)][:].rearrange("p h u x -> p h x u"))
 
@@ -246,13 +248,7 @@ def tile_localselfattention_pa_t_kernel(tc, q, k_scaled, hidden_states, Wv, out)
 
         def invert_sums(c, j):
             inverse[(c, j)] = work.tile([P, 2 * HEADS], F32, bufs=3, name="inverse")
-            sums = row_sums[(c, j)][:].rearrange("p t h s -> p (t h) s")
-            if c == 0:
-                nc.vector.reciprocal(out=inverse[(c, j)][:], in_=sums[:, :, 0])
-            else:
-                total = work.tile([P, 2 * HEADS], F32, bufs=3, name="total")
-                nc.vector.tensor_reduce(out=total[:], in_=sums, axis=AXIS.X, op=ALU.add)
-                nc.vector.reciprocal(out=inverse[(c, j)][:], in_=total[:])
+            nc.vector.reciprocal(out=inverse[(c, j)][:], in_=row_sums[(c, j)][:])
 
         def finish(c, j):
             result = work.tile([P, 2, WIDTH], F32, bufs=3, name="result")
@@ -272,7 +268,7 @@ def tile_localselfattention_pa_t_kernel(tc, q, k_scaled, hidden_states, Wv, out)
                 if i % 2 == 1:
                     finish(c, i // 2)
             if 0 <= k + 1 < n:
-                maxima(k + 1)
+                move_own(k + 1)
             if 0 <= k < n:
                 exponentials(k)
             if 0 <= k - 1 < n and units[k - 1][2] == HEADS - 1:
@@ -282,8 +278,9 @@ def tile_localselfattention_pa_t_kernel(tc, q, k_scaled, hidden_states, Wv, out)
             if 0 <= k + LEAD - 1 < n:
                 prepare_on_vector((k + LEAD - 1) // pieces, (k + LEAD - 1) % pieces)
             if 0 <= k + 2 < n:
-                scores_own(k + 2)
                 scores_prev(k + 2)
+                move_prev(k + 2)
+                scores_own(k + 2)
             if 0 <= k - 1 < n and units[k - 1][2] == HEADS - 1:
                 regroup(units[k - 1][0], units[k - 1][1])
             if 0 <= k - 2 < n and units[k - 2][2] == HEADS - 1:

@@ -24,7 +24,7 @@ N_CHUNKS = SEQ // CHUNK
 TILES = CHUNK // P
 HID_PASSES = HID // CHUNK
 MASKED = -1.0e9
-LEAD = 6
+LEAD = 10
 
 SCORE_CELLS = HEADS * (2 * N_CHUNKS - 1) * CHUNK * CHUNK
 FLOPS = 2 * SEQ * HID * WIDTH + 2 * 2 * SCORE_CELLS * DH
@@ -41,24 +41,25 @@ def tile_localselfattention_pa_t_kernel(tc, q, k_scaled, hidden_states, Wv, out)
         const = ctx.enter_context(tc.tile_pool(name="const", bufs=1))
         raw = ctx.enter_context(tc.tile_pool(name="raw", bufs=1))
         work = ctx.enter_context(tc.tile_pool(name="work", bufs=2))
-        psum = ctx.enter_context(tc.psum_pool(name="psum", bufs=7))
+        psum = ctx.enter_context(tc.psum_pool(name="psum", bufs=3))
+        psum_sc = ctx.enter_context(tc.psum_pool(name="psum_sc", bufs=2))
         psum_sum = ctx.enter_context(tc.psum_pool(name="psum_sum", bufs=1))
 
         q_raw, k_raw, h_raw = {}, {}, {}
         w_raw = raw.tile([P, HID_PASSES * PACK * WIDTH], BF16)
         for c in range(N_CHUNKS):
-            k_raw[c] = raw.tile([P, TILES, WIDTH], BF16, name="k_raw%d" % c)
-            nc.sync.dma_start(out=k_raw[c][:], in_=k_rows[c])
-            q_raw[c] = raw.tile([P, TILES, WIDTH], BF16, name="q_raw%d" % c)
-            nc.sync.dma_start(out=q_raw[c][:], in_=q_rows[c])
+            h_raw[c] = raw.tile([P, TILES * HID], BF16, name="h_raw%d" % c)
+            for u in range(TILES // 2):
+                nc.sync.dma_start(out=h_raw[c][:, 2 * u * HID:2 * (u + 1) * HID], in_=h_rows[c][:, u, :])
             if c == 0:
                 nc.sync.dma_start(
                     out=w_raw[:].rearrange("p (s x) -> p s x", s=HID_PASSES * 2),
                     in_=Wv.rearrange("(s p e) n -> p s (e n)", p=P, e=2),
                 )
-            h_raw[c] = raw.tile([P, TILES * HID], BF16, name="h_raw%d" % c)
-            for u in range(TILES // 2):
-                nc.sync.dma_start(out=h_raw[c][:, 2 * u * HID:2 * (u + 1) * HID], in_=h_rows[c][:, u, :])
+            k_raw[c] = raw.tile([P, TILES, WIDTH], BF16, name="k_raw%d" % c)
+            nc.sync.dma_start(out=k_raw[c][:], in_=k_rows[c])
+            q_raw[c] = raw.tile([P, TILES, WIDTH], BF16, name="q_raw%d" % c)
+            nc.sync.dma_start(out=q_raw[c][:], in_=q_rows[c])
 
         ident_bf = const.tile([P, P], BF16)
         make_identity(nc, ident_bf[:])
@@ -92,14 +93,14 @@ def tile_localselfattention_pa_t_kernel(tc, q, k_scaled, hidden_states, Wv, out)
         prep_bank = {}
 
         def prepare_on_tensor(c, piece):
-            if piece < 2:
-                src = k_raw[c] if piece == 0 else q_raw[c]
+            if piece in (4, 5):
+                src = k_raw[c] if piece == 4 else q_raw[c]
                 bank = psum.tile([P, HEADS, TILES, P], BF16, tag="bank", name="qk_bank")
                 for h in range(HEADS):
                     for i in range(TILES):
                         nc.tensor.transpose(bank[:, h, i, :], src[:, i, h * DH:(h + 1) * DH], ident_bf[:])
-            elif piece < 2 + TILES:
-                t = piece - 2
+            elif piece < TILES:
+                t = piece
                 words = h_raw[c][:].bitcast(F32)
                 bank = psum.tile([P, HID_PASSES, 2, P], F32, tag="bank", name="h_bank")
                 for g in range(HID_PASSES):
@@ -121,42 +122,47 @@ def tile_localselfattention_pa_t_kernel(tc, q, k_scaled, hidden_states, Wv, out)
                         )
             prep_bank[(c, piece)] = bank
 
-        def prepare_on_vector(c, piece):
+        def prepare_copy(c, piece):
             bank = prep_bank[(c, piece)]
-            if piece < 2:
-                flipped = work.tile([P, HEADS, CHUNK], BF16, tag="k_t" if piece == 0 else "q_t",
-                                    bufs=3 if piece == 0 else 2, name="flipped")
+            if piece in (4, 5):
+                flipped = work.tile([P, HEADS, CHUNK], BF16, tag="k_t" if piece == 4 else "q_t",
+                                    bufs=3 if piece == 4 else 2, name="flipped")
                 nc.scalar.copy(out=flipped[:], in_=bank[:].rearrange("p h i x -> p h (i x)"))
-                if piece == 0:
+                if piece == 4:
                     k_t[c] = flipped
                 else:
                     q_t[c] = flipped
-            elif piece < 2 + TILES:
-                t = piece - 2
+            elif piece < TILES:
+                t = piece
                 if t == 0:
                     h_grp[c] = work.tile([P, TILES * HID_PASSES * P * PACK], BF16, align_bytes=64, name="h_grp")
-                    h_codes[c] = work.tile([P, TILES * HID_PASSES * P], U32, align_bytes=64, name="h_codes")
-                    h_scales[c] = work.tile([P, TILES * HID_PASSES * P], U8, align_bytes=64, name="h_scales")
                 grouped = h_grp[c][:].bitcast(F32).rearrange(
                     "p (t g x a) -> p t g x a", t=TILES, g=HID_PASSES, a=2)
                 nc.scalar.copy(out=grouped[:, t], in_=bank[:].rearrange("p g a x -> p g x a"))
+            else:
+                h = piece - 2 - TILES
+                if h == 0:
+                    v_grp[c] = work.tile([P, WIDTH * PACK], BF16, align_bytes=64, name="v_grp")
+                nc.scalar.copy(
+                    out=v_grp[c][:, h * DH * PACK:(h + 1) * DH * PACK].rearrange("p (d t) -> p d t", t=PACK),
+                    in_=bank[:].rearrange("p t d -> p d t"),
+                )
+
+        def prepare_quantise(c, piece):
+            if piece < TILES:
+                t = piece
+                if t == 0:
+                    h_codes[c] = work.tile([P, TILES * HID_PASSES * P], U32, align_bytes=64, name="h_codes")
+                    h_scales[c] = work.tile([P, TILES * HID_PASSES * P], U8, align_bytes=64, name="h_scales")
                 words = slice(t * HID_PASSES * P, (t + 1) * HID_PASSES * P)
                 nc.vector.quantize_mx(
                     out=h_codes[c][:, words].bitcast(FP8X4), scales=h_scales[c][:, words],
                     in_=h_grp[c][:, t * HID_PASSES * P * PACK:(t + 1) * HID_PASSES * P * PACK],
                 )
-            else:
-                h = piece - 2 - TILES
-                if h == 0:
-                    v_grp[c] = work.tile([P, WIDTH * PACK], BF16, align_bytes=64, name="v_grp")
-                    v_codes[c] = work.tile([P, WIDTH], U32, align_bytes=64, bufs=3, name="v_codes")
-                    v_scales[c] = work.tile([P, WIDTH], U8, align_bytes=64, bufs=3, name="v_scales")
-                nc.scalar.copy(
-                    out=v_grp[c][:, h * DH * PACK:(h + 1) * DH * PACK].rearrange("p (d t) -> p d t", t=PACK),
-                    in_=bank[:].rearrange("p t d -> p d t"),
-                )
-                if h == HEADS - 1:
-                    nc.vector.quantize_mx(out=v_codes[c][:].bitcast(FP8X4), scales=v_scales[c][:], in_=v_grp[c][:])
+            elif piece == 2 + TILES + HEADS - 1:
+                v_codes[c] = work.tile([P, WIDTH], U32, align_bytes=64, bufs=3, name="v_codes")
+                v_scales[c] = work.tile([P, WIDTH], U8, align_bytes=64, bufs=3, name="v_scales")
+                nc.vector.quantize_mx(out=v_codes[c][:].bitcast(FP8X4), scales=v_scales[c][:], in_=v_grp[c][:])
 
         units = [(c, i, h) for c in range(N_CHUNKS) for i in range(TILES) for h in range(HEADS)]
         s_own, s_prev, neg_scores, neg_max, own_bank, prev_bank, e_grp, e_codes, e_scales = {}, {}, {}, {}, {}, {}, {}, {}, {}
@@ -166,20 +172,20 @@ def tile_localselfattention_pa_t_kernel(tc, q, k_scaled, hidden_states, Wv, out)
             c, i, h = units[u]
             seen = (i + 1) * P
             queries = q_t[c][:, h, i * P:(i + 1) * P]
-            s_own[u] = psum.tile([P, CHUNK], F32, tag="bank", name="s_own")
+            s_own[u] = psum_sc.tile([P, CHUNK], F32, tag="own", bufs=2, name="s_own")
             nc.tensor.matmul(s_own[u][:, :seen], lhsT=queries, rhs=k_t[c][:, h, :seen], start=True, stop=False)
             nc.tensor.matmul(s_own[u][:, i * P:seen], lhsT=ident_bf[:], rhs=mask_bf[:], start=False, stop=True)
 
         def scores_prev(u):
             c, i, h = units[u]
             if c > 0:
-                s_prev[u] = psum.tile([P, CHUNK], F32, tag="bank", name="s_prev")
+                s_prev[u] = psum_sc.tile([P, CHUNK], F32, tag="prev", bufs=2, name="s_prev")
                 nc.tensor.matmul(s_prev[u][:], lhsT=q_t[c][:, h, i * P:(i + 1) * P], rhs=k_t[c - 1][:, h, :],
                                  start=True, stop=True)
 
         def move_prev(u):
-            neg_scores[u] = work.tile([P, 2 * CHUNK], F32, bufs=4, name="neg_scores")
-            neg_max[u] = work.tile([P, 2], F32, bufs=4, name="neg_max")
+            neg_scores[u] = work.tile([P, 2 * CHUNK], F32, bufs=5, name="neg_scores")
+            neg_max[u] = work.tile([P, 2], F32, bufs=6, name="neg_max")
             if units[u][0] > 0:
                 nc.vector.tensor_scalar(out=neg_scores[u][:, :CHUNK], in0=s_prev[u][:], scalar1=-1.0, scalar2=None,
                                         op0=ALU.mult, op1=ALU.min, accum_out=neg_max[u][:, 0:1])
@@ -259,34 +265,42 @@ def tile_localselfattention_pa_t_kernel(tc, q, k_scaled, hidden_states, Wv, out)
             )
             nc.sync.dma_start(out=out_rows[c * TILES // 2 + j], in_=result[:])
 
-        pieces = 2 + TILES + HEADS
+        pieces = TILES + 2 + HEADS
         assert pieces == TILES * HEADS
         n = len(units)
-        for k in range(-LEAD, n + 4):
-            if 0 <= k - 4 and units[k - 4][2] == HEADS - 1:
-                c, i, h = units[k - 4]
-                if i % 2 == 1:
-                    finish(c, i // 2)
-            if 0 <= k + 1 < n:
-                move_own(k + 1)
+
+        def tile_done(u):
+            return 0 <= u < n and units[u][2] == HEADS - 1
+
+        def pair_done(u):
+            return tile_done(u) and units[u][1] % 2 == 1
+
+        ctx.enter_context(tc.manual_schedule())
+        for k in range(-LEAD, n + 5):
+            if pair_done(k - 5):
+                finish(units[k - 5][0], units[k - 5][1] // 2)
+            if tile_done(k - 4):
+                weighted_sum(units[k - 4][0], units[k - 4][1])
+            if pair_done(k - 3):
+                invert_sums(units[k - 3][0], units[k - 3][1] // 2)
+            if tile_done(k - 3):
+                quantise(units[k - 3][0], units[k - 3][1])
+            if tile_done(k - 2):
+                regroup(units[k - 2][0], units[k - 2][1])
+            if 0 <= k + LEAD - 2 < n:
+                prepare_quantise((k + LEAD - 2) // pieces, (k + LEAD - 2) % pieces)
+            if 0 <= k + LEAD - 1 < n:
+                prepare_copy((k + LEAD - 1) // pieces, (k + LEAD - 1) % pieces)
             if 0 <= k < n:
                 exponentials(k)
-            if 0 <= k - 1 < n and units[k - 1][2] == HEADS - 1:
-                flip(units[k - 1][0], units[k - 1][1])
-            if 0 <= k - 3 < n and units[k - 3][2] == HEADS - 1:
-                weighted_sum(units[k - 3][0], units[k - 3][1])
-            if 0 <= k + LEAD - 1 < n:
-                prepare_on_vector((k + LEAD - 1) // pieces, (k + LEAD - 1) % pieces)
+            if 0 <= k + 1 < n:
+                move_own(k + 1)
             if 0 <= k + 2 < n:
-                scores_prev(k + 2)
                 move_prev(k + 2)
                 scores_own(k + 2)
-            if 0 <= k - 1 < n and units[k - 1][2] == HEADS - 1:
-                regroup(units[k - 1][0], units[k - 1][1])
-            if 0 <= k - 2 < n and units[k - 2][2] == HEADS - 1:
-                quantise(units[k - 2][0], units[k - 2][1])
-                c, i, h = units[k - 2]
-                if i % 2 == 1:
-                    invert_sums(c, i // 2)
+            if 0 <= k + 3 < n:
+                scores_prev(k + 3)
+            if tile_done(k - 1):
+                flip(units[k - 1][0], units[k - 1][1])
             if 0 <= k + LEAD < n:
                 prepare_on_tensor((k + LEAD) // pieces, (k + LEAD) % pieces)

@@ -6,11 +6,11 @@ from concourse.masks import make_identity
 F32 = mybir.dt.float32
 BF16 = mybir.dt.bfloat16
 U32 = mybir.dt.uint32
+I32 = mybir.dt.int32
 U8 = mybir.dt.uint8
 FP8X4 = mybir.dt.float8_e4m3fn_x4
 ACT = mybir.ActivationFunctionType
 ALU = mybir.AluOpType
-AXIS = mybir.AxisListType
 
 P = 128
 PACK = 4
@@ -24,7 +24,8 @@ N_CHUNKS = SEQ // CHUNK
 TILES = CHUNK // P
 HID_PASSES = HID // CHUNK
 MASKED = -1.0e9
-LEAD = 10
+OWN_ON_SCALAR = (2, 1)
+LEAD = 5
 
 SCORE_CELLS = HEADS * (2 * N_CHUNKS - 1) * CHUNK * CHUNK
 FLOPS = 2 * SEQ * HID * WIDTH + 2 * 2 * SCORE_CELLS * DH
@@ -33,33 +34,38 @@ FLOPS = 2 * SEQ * HID * WIDTH + 2 * 2 * SCORE_CELLS * DH
 def tile_localselfattention_pa_t_kernel(tc, q, k_scaled, hidden_states, Wv, out):
     nc = tc.nc
     q_rows = q.flatten_outer_dims().rearrange("(c i p) w -> c p i w", i=TILES, p=P)
-    k_rows = k_scaled.flatten_outer_dims().rearrange("(c i p) w -> c p i w", i=TILES, p=P)
-    h_rows = hidden_states.flatten_outer_dims().rearrange("(c u p e) k -> c p u (e k)", u=TILES // 2, p=P, e=2)
-    out_rows = out.flatten_outer_dims().rearrange("(n j p) w -> n p j w", j=2, p=P)
+    k_rows = k_scaled.flatten_outer_dims().rearrange("(c p t) w -> c p t w", t=PACK, p=P)
+    h_rows = hidden_states.flatten_outer_dims().rearrange("(c p t) k -> c p t k", t=PACK, p=P)
+    out_rows = out.flatten_outer_dims().rearrange("(c a b p) w -> c b p a w", a=2, b=2, p=P)
 
     with ExitStack() as ctx:
         const = ctx.enter_context(tc.tile_pool(name="const", bufs=1))
         raw = ctx.enter_context(tc.tile_pool(name="raw", bufs=1))
         work = ctx.enter_context(tc.tile_pool(name="work", bufs=2))
         psum = ctx.enter_context(tc.psum_pool(name="psum", bufs=3))
-        psum_sc = ctx.enter_context(tc.psum_pool(name="psum_sc", bufs=2))
+        psum_scores = ctx.enter_context(tc.psum_pool(name="psum_scores", bufs=2))
         psum_sum = ctx.enter_context(tc.psum_pool(name="psum_sum", bufs=1))
 
         q_raw, k_raw, h_raw = {}, {}, {}
         w_raw = raw.tile([P, HID_PASSES * PACK * WIDTH], BF16)
-        for c in range(N_CHUNKS):
-            h_raw[c] = raw.tile([P, TILES * HID], BF16, name="h_raw%d" % c)
-            for u in range(TILES // 2):
-                nc.sync.dma_start(out=h_raw[c][:, 2 * u * HID:2 * (u + 1) * HID], in_=h_rows[c][:, u, :])
+
+        def load(c):
+            k_raw[c] = raw.tile([P, PACK, WIDTH], BF16, name="k_raw%d" % c)
+            nc.sync.dma_start(out=k_raw[c][:], in_=k_rows[c])
+            q_raw[c] = raw.tile([P, TILES, WIDTH], BF16, name="q_raw%d" % c)
+            nc.sync.dma_start(out=q_raw[c][:], in_=q_rows[c])
+            h_raw[c] = raw.tile([P, PACK * HID], BF16, name="h_raw%d" % c)
+            for t in range(0, PACK, 2):
+                nc.sync.dma_start(out=h_raw[c][:, t * HID:(t + 2) * HID].rearrange("p (t k) -> p t k", t=2),
+                                  in_=h_rows[c][:, t:t + 2, :])
             if c == 0:
                 nc.sync.dma_start(
                     out=w_raw[:].rearrange("p (s x) -> p s x", s=HID_PASSES * 2),
                     in_=Wv.rearrange("(s p e) n -> p s (e n)", p=P, e=2),
                 )
-            k_raw[c] = raw.tile([P, TILES, WIDTH], BF16, name="k_raw%d" % c)
-            nc.sync.dma_start(out=k_raw[c][:], in_=k_rows[c])
-            q_raw[c] = raw.tile([P, TILES, WIDTH], BF16, name="q_raw%d" % c)
-            nc.sync.dma_start(out=q_raw[c][:], in_=q_rows[c])
+
+        load(0)
+        load(1)
 
         ident_bf = const.tile([P, P], BF16)
         make_identity(nc, ident_bf[:])
@@ -71,185 +77,263 @@ def tile_localselfattention_pa_t_kernel(tc, q, k_scaled, hidden_states, Wv, out)
             out=mask_f32[:], in_=mask_f32[:], compare_op=ALU.is_ge, fill=MASKED,
             base=0, pattern=[[-1, P]], channel_multiplier=1,
         )
-        mask_bf = const.tile([P, P], BF16)
-        nc.vector.tensor_copy(out=mask_bf[:], in_=mask_f32[:])
-        e_rows = {}
-        for i in range(TILES):
-            for h in range(HEADS):
-                e_rows[(i, h)] = const.tile([P, 2 * CHUNK], BF16, align_bytes=64, name="e_rows_%d_%d" % (i, h))
-                if i < TILES - 1:
-                    nc.vector.memset(e_rows[(i, h)][:, CHUNK + (i + 1) * P:], 0.0)
+        mask_bf = const.tile([P, PACK, P // PACK], BF16)
+        nc.vector.tensor_copy(out=mask_bf[:], in_=mask_f32[:].rearrange("p (x t) -> p t x", t=PACK))
+
+        half = CHUNK // 2
+        rows = {}
+        for i, h, width in ((2, 0, 3 * half), (2, 1, 3 * half), (1, 0, 3 * half), (3, 0, 2 * half), (3, 1, 2 * half)):
+            rows[(i, h)] = const.tile([P, 2, width], BF16, align_bytes=64, name="rows_%d_%d" % (i, h))
+
+        def place(i, h):
+            own = (i + 1) * P // 2
+            if i == 0:
+                return rows[(2, h)], 2 * half - own, 2 * half
+            if i == 1 and h == 1:
+                return rows[(1, 0)], 2 * half - own, 2 * half
+            return rows[(i, h)], half, 0
+
+        v_front, v_back, v_half, v_back_scales, v_half_scales = {}, {}, {}, {}, {}
+        for b in range(2):
+            v_front[b] = const.tile([P, WIDTH], U32, align_bytes=64, name="v_front%d" % b)
+            v_back[b] = const.tile([P, WIDTH], U32, align_bytes=64, name="v_back%d" % b)
+            v_half[b] = const.tile([P, WIDTH], U32, align_bytes=64, name="v_half%d" % b)
+            v_back_scales[b] = const.tile([P, WIDTH], U8, align_bytes=64, name="v_back_scales%d" % b)
+            v_half_scales[b] = const.tile([P, DH], U8, align_bytes=64, name="v_half_scales%d" % b)
+            for t in (v_front[b], v_back[b], v_half[b]):
+                nc.gpsimd.memset(t[:], 0)
+            for t in (v_back_scales[b], v_half_scales[b]):
+                nc.gpsimd.memset(t[:].bitcast(I32), 0)
 
         w_grp = const.tile([P, HID_PASSES * WIDTH * PACK], BF16, align_bytes=64)
         w_codes = const.tile([P, HID_PASSES * WIDTH], U32, align_bytes=64)
         w_scales = const.tile([P, HID_PASSES * WIDTH], U8, align_bytes=64)
-        nc.vector.tensor_copy(
-            out=w_grp[:].rearrange("p (g n t) -> p g n t", g=HID_PASSES, t=PACK),
-            in_=w_raw[:].rearrange("p (g t n) -> p g n t", g=HID_PASSES, t=PACK),
-        )
-        nc.vector.quantize_mx(out=w_codes[:].bitcast(FP8X4), scales=w_scales[:], in_=w_grp[:])
+
+        def group_weights():
+            nc.vector.tensor_copy(
+                out=w_grp[:].rearrange("p (g n t) -> p g n t", g=HID_PASSES, t=PACK),
+                in_=w_raw[:].rearrange("p (g t n) -> p g n t", g=HID_PASSES, t=PACK),
+            )
+
+        def quantise_weights():
+            nc.vector.quantize_mx(out=w_codes[:].bitcast(FP8X4), scales=w_scales[:], in_=w_grp[:])
 
         k_t, q_t, h_grp, h_codes, h_scales, v_grp, v_codes, v_scales = {}, {}, {}, {}, {}, {}, {}, {}
         prep_bank = {}
 
-        def prepare_on_tensor(c, piece):
-            if piece in (4, 5):
-                src = k_raw[c] if piece == 4 else q_raw[c]
-                bank = psum.tile([P, HEADS, TILES, P], BF16, tag="bank", name="qk_bank")
-                for h in range(HEADS):
-                    for i in range(TILES):
-                        nc.tensor.transpose(bank[:, h, i, :], src[:, i, h * DH:(h + 1) * DH], ident_bf[:])
-            elif piece < TILES:
-                t = piece
-                words = h_raw[c][:].bitcast(F32)
-                bank = psum.tile([P, HID_PASSES, 2, P], F32, tag="bank", name="h_bank")
+        def transpose_keys_or_queries(c, src, name):
+            bank = psum.tile([P, HEADS, TILES, P], BF16, tag="bank", name="qk_bank")
+            for h in range(HEADS):
+                for i in range(TILES):
+                    nc.tensor.transpose(bank[:, h, i, :], src[:, i, h * DH:(h + 1) * DH], ident_bf[:])
+            prep_bank[(c, name)] = bank
+
+        def transpose_hidden(c, t):
+            words = h_raw[c][:].bitcast(F32)
+            bank = psum.tile([P, HID_PASSES, 2, P], F32, tag="bank", name="h_bank")
+            for g in range(HID_PASSES):
+                for a in range(2):
+                    first = (t * HID_PASSES * 2 + g * 2 + a) * P
+                    nc.tensor.transpose(bank[:, g, a, :], words[:, first:first + P], ident_f32[:])
+            prep_bank[(c, "h", t)] = bank
+
+        def multiply_values(c, h):
+            bank = psum.tile([P, PACK, DH], F32, tag="bank", name="v_bank")
+            for t in range(PACK):
                 for g in range(HID_PASSES):
-                    for a in range(2):
-                        first = (t * HID_PASSES * 2 + g * 2 + a) * P
-                        nc.tensor.transpose(bank[:, g, a, :], words[:, first:first + P], ident_f32[:])
-            else:
-                h = piece - 2 - TILES
-                bank = psum.tile([P, TILES, DH], F32, tag="bank", name="v_bank")
-                for t in range(TILES):
-                    for g in range(HID_PASSES):
-                        rows = slice((t * HID_PASSES + g) * P, (t * HID_PASSES + g + 1) * P)
-                        cols = slice(g * WIDTH + h * DH, g * WIDTH + (h + 1) * DH)
-                        nc.tensor.matmul_mx(
-                            out=bank[:, t, :],
-                            lhsT=h_codes[c][:, rows].bitcast(FP8X4), lhsT_scale=h_scales[c][:, rows],
-                            rhs=w_codes[:, cols].bitcast(FP8X4), rhs_scale=w_scales[:, cols],
-                            start=(g == 0), stop=(g == HID_PASSES - 1),
-                        )
-            prep_bank[(c, piece)] = bank
+                    r = slice((t * HID_PASSES + g) * P, (t * HID_PASSES + g + 1) * P)
+                    cols = slice(g * WIDTH + h * DH, g * WIDTH + (h + 1) * DH)
+                    nc.tensor.matmul_mx(
+                        out=bank[:, t, :],
+                        lhsT=h_codes[c][:, r].bitcast(FP8X4), lhsT_scale=h_scales[c][:, r],
+                        rhs=w_codes[:, cols].bitcast(FP8X4), rhs_scale=w_scales[:, cols],
+                        start=(g == 0), stop=(g == HID_PASSES - 1),
+                    )
+            prep_bank[(c, "v", h)] = bank
 
-        def prepare_copy(c, piece):
-            bank = prep_bank[(c, piece)]
-            if piece in (4, 5):
-                flipped = work.tile([P, HEADS, CHUNK], BF16, tag="k_t" if piece == 4 else "q_t",
-                                    bufs=3 if piece == 4 else 2, name="flipped")
-                nc.scalar.copy(out=flipped[:], in_=bank[:].rearrange("p h i x -> p h (i x)"))
-                if piece == 4:
-                    k_t[c] = flipped
-                else:
-                    q_t[c] = flipped
-            elif piece < TILES:
-                t = piece
-                if t == 0:
-                    h_grp[c] = work.tile([P, TILES * HID_PASSES * P * PACK], BF16, align_bytes=64, name="h_grp")
-                grouped = h_grp[c][:].bitcast(F32).rearrange(
-                    "p (t g x a) -> p t g x a", t=TILES, g=HID_PASSES, a=2)
-                nc.scalar.copy(out=grouped[:, t], in_=bank[:].rearrange("p g a x -> p g x a"))
-            else:
-                h = piece - 2 - TILES
-                if h == 0:
-                    v_grp[c] = work.tile([P, WIDTH * PACK], BF16, align_bytes=64, name="v_grp")
-                nc.scalar.copy(
-                    out=v_grp[c][:, h * DH * PACK:(h + 1) * DH * PACK].rearrange("p (d t) -> p d t", t=PACK),
-                    in_=bank[:].rearrange("p t d -> p d t"),
-                )
+        def copy_keys_or_queries(c, name):
+            into, bufs = (k_t, 3) if name == "k" else (q_t, 2)
+            into[c] = work.tile([P, HEADS, TILES, P], BF16, tag=name + "_t", bufs=bufs, name="turned")
+            nc.scalar.copy(out=into[c][:], in_=prep_bank[(c, name)][:])
 
-        def prepare_quantise(c, piece):
-            if piece < TILES:
-                t = piece
-                if t == 0:
-                    h_codes[c] = work.tile([P, TILES * HID_PASSES * P], U32, align_bytes=64, name="h_codes")
-                    h_scales[c] = work.tile([P, TILES * HID_PASSES * P], U8, align_bytes=64, name="h_scales")
-                words = slice(t * HID_PASSES * P, (t + 1) * HID_PASSES * P)
-                nc.vector.quantize_mx(
-                    out=h_codes[c][:, words].bitcast(FP8X4), scales=h_scales[c][:, words],
-                    in_=h_grp[c][:, t * HID_PASSES * P * PACK:(t + 1) * HID_PASSES * P * PACK],
-                )
-            elif piece == 2 + TILES + HEADS - 1:
-                v_codes[c] = work.tile([P, WIDTH], U32, align_bytes=64, bufs=3, name="v_codes")
-                v_scales[c] = work.tile([P, WIDTH], U8, align_bytes=64, bufs=3, name="v_scales")
-                nc.vector.quantize_mx(out=v_codes[c][:].bitcast(FP8X4), scales=v_scales[c][:], in_=v_grp[c][:])
+        def copy_hidden(c, t):
+            if t == 0:
+                h_grp[c] = work.tile([P, PACK * HID_PASSES * P * PACK], BF16, align_bytes=64, name="h_grp")
+            grouped = h_grp[c][:].bitcast(F32).rearrange("p (t g x a) -> p t g x a", t=PACK, g=HID_PASSES, a=2)
+            nc.scalar.copy(out=grouped[:, t], in_=prep_bank[(c, "h", t)][:].rearrange("p g a x -> p g x a"))
 
-        units = [(c, i, h) for c in range(N_CHUNKS) for i in range(TILES) for h in range(HEADS)]
+        def copy_values(c, h):
+            if h == 0:
+                v_grp[c] = work.tile([P, WIDTH * PACK], BF16, align_bytes=64, name="v_grp")
+            nc.scalar.copy(
+                out=v_grp[c][:, h * DH * PACK:(h + 1) * DH * PACK].rearrange("p (d t) -> p d t", t=PACK),
+                in_=prep_bank[(c, "v", h)][:].rearrange("p t d -> p d t"),
+            )
+
+        def quantise_hidden(c, t):
+            if t == 0:
+                h_codes[c] = work.tile([P, PACK * HID_PASSES * P], U32, align_bytes=64, name="h_codes")
+                h_scales[c] = work.tile([P, PACK * HID_PASSES * P], U8, align_bytes=64, name="h_scales")
+            words = slice(t * HID_PASSES * P, (t + 1) * HID_PASSES * P)
+            nc.vector.quantize_mx(
+                out=h_codes[c][:, words].bitcast(FP8X4), scales=h_scales[c][:, words],
+                in_=h_grp[c][:, t * HID_PASSES * P * PACK:(t + 1) * HID_PASSES * P * PACK],
+            )
+
+        def quantise_values(c):
+            v_codes[c] = work.tile([P, WIDTH], U32, align_bytes=64, bufs=3, name="v_codes")
+            v_scales[c] = work.tile([P, WIDTH], U8, align_bytes=64, bufs=3, name="v_scales")
+            nc.vector.quantize_mx(out=v_codes[c][:].bitcast(FP8X4), scales=v_scales[c][:], in_=v_grp[c][:])
+
+        def spread_values(c):
+            b = c % 2
+            codes, scales = v_codes[c], v_scales[c]
+            for dst, src in (
+                (v_front[b][:96, :], codes[:96, :]),
+                (v_back[b][96:, :], codes[:32, :]),
+                (v_back_scales[b][96:100, :], scales[0:4, :]),
+                (v_half[b][:64, :DH], codes[:64, :DH]),
+                (v_half[b][64:, DH:], codes[:64, DH:]),
+                (v_half_scales[b][64:68, :], scales[0:4, DH:]),
+                (v_half_scales[b][96:100, :], scales[32:36, DH:]),
+            ):
+                nc.sync.dma_start(out=dst.bitcast(I32), in_=src.bitcast(I32))
+
+        units = [(c, i, h) for c in range(N_CHUNKS) for i in (0, 2, 1, 3) for h in range(HEADS)]
         s_own, s_prev, neg_scores, neg_max, own_bank, prev_bank, e_grp, e_codes, e_scales = {}, {}, {}, {}, {}, {}, {}, {}, {}
         row_sums, inverse, acc = {}, {}, {}
 
         def scores_own(u):
             c, i, h = units[u]
-            seen = (i + 1) * P
-            queries = q_t[c][:, h, i * P:(i + 1) * P]
-            s_own[u] = psum_sc.tile([P, CHUNK], F32, tag="own", bufs=2, name="s_own")
-            nc.tensor.matmul(s_own[u][:, :seen], lhsT=queries, rhs=k_t[c][:, h, :seen], start=True, stop=False)
-            nc.tensor.matmul(s_own[u][:, i * P:seen], lhsT=ident_bf[:], rhs=mask_bf[:], start=False, stop=True)
+            seen = (i + 1) * P // PACK
+            queries = q_t[c][:, h, i, :]
+            s_own[u] = psum_scores.tile([P, CHUNK], F32, tag="own", name="s_own")
+            scores = s_own[u][:, :PACK * seen].rearrange("p (t x) -> p t x", t=PACK)
+            nc.tensor.matmul(scores, lhsT=queries, rhs=k_t[c][:, h, :, :seen], start=True, stop=False)
+            nc.tensor.matmul(scores[:, :, seen - P // PACK:], lhsT=ident_bf[:], rhs=mask_bf[:], start=False, stop=True)
 
         def scores_prev(u):
             c, i, h = units[u]
             if c > 0:
-                s_prev[u] = psum_sc.tile([P, CHUNK], F32, tag="prev", bufs=2, name="s_prev")
-                nc.tensor.matmul(s_prev[u][:], lhsT=q_t[c][:, h, i * P:(i + 1) * P], rhs=k_t[c - 1][:, h, :],
-                                 start=True, stop=True)
+                s_prev[u] = psum_scores.tile([P, PACK, P], F32, tag="prev", name="s_prev")
+                nc.tensor.matmul(s_prev[u][:], lhsT=q_t[c][:, h, i, :], rhs=k_t[c - 1][:, h, :, :], start=True, stop=True)
+
+        def move(u, scores, column, initial, result):
+            seen = scores.shape[2]
+            nc.vector.tensor_scalar(
+                out=neg_scores[u][:, :, column:column + 2 * seen].rearrange("p u (x e) -> p u x e", e=2),
+                in0=scores.rearrange("p (u e) x -> p u x e", e=2),
+                scalar1=-1.0, scalar2=initial, op0=ALU.mult, op1=ALU.min, accum_out=result,
+            )
+
+        def columns(u):
+            c, i, h = units[u]
+            own = (i + 1) * P // 2
+            first_own, first_prev = place(i, h)[1:]
+            if c == 0:
+                return 0, None, own
+            return (0, own, own + half) if first_own < first_prev else (half, 0, own + half)
 
         def move_prev(u):
-            neg_scores[u] = work.tile([P, 2 * CHUNK], F32, bufs=5, name="neg_scores")
+            neg_scores[u] = work.tile([P, 2, CHUNK], F32, bufs=5, name="neg_scores")
             neg_max[u] = work.tile([P, 2], F32, bufs=6, name="neg_max")
             if units[u][0] > 0:
-                nc.vector.tensor_scalar(out=neg_scores[u][:, :CHUNK], in0=s_prev[u][:], scalar1=-1.0, scalar2=None,
-                                        op0=ALU.mult, op1=ALU.min, accum_out=neg_max[u][:, 0:1])
+                move(u, s_prev[u][:], columns(u)[1], None, neg_max[u][:, 0:1])
 
         def move_own(u):
             c, i, h = units[u]
-            seen = (i + 1) * P
-            nc.vector.tensor_scalar(out=neg_scores[u][:, CHUNK:CHUNK + seen], in0=s_own[u][:, :seen], scalar1=-1.0,
-                                    scalar2=neg_max[u][:, 0:1] if c > 0 else None,
-                                    op0=ALU.mult, op1=ALU.min, accum_out=neg_max[u][:, 1:2])
+            scores = s_own[u][:, :(i + 1) * P].rearrange("p (t x) -> p t x", t=PACK)
+            move(u, scores, columns(u)[0], neg_max[u][:, 0:1] if c > 0 else None, neg_max[u][:, 1:2])
 
         def exponentials(u):
             c, i, h = units[u]
-            if i % 2 == 0 and h == 0:
-                row_sums[(c, i // 2)] = work.tile([P, 2 * HEADS], F32, bufs=3, name="row_sums")
-            keys = slice(CHUNK if c == 0 else 0, CHUNK + (i + 1) * P)
-            column = (i % 2) * HEADS + h
-            nc.scalar.activation(out=e_rows[(i, h)][:, keys], in_=neg_scores[u][:, keys], func=ACT.Exp,
-                                 bias=neg_max[u][:, 1:2], scale=-1.0,
-                                 accum_out=row_sums[(c, i // 2)][:, column:column + 1])
+            pair = (c, i % 2)
+            if i < 2 and h == 0:
+                row_sums[pair] = work.tile([P, 2 * HEADS], F32, bufs=3, name="row_sums")
+            into, first_own, first_prev = place(i, h)
+            first = first_own if c == 0 else min(first_own, first_prev)
+            width = columns(u)[2]
+            column = (i // 2) * HEADS + h
+            nc.scalar.activation(out=into[:, :, first:first + width], in_=neg_scores[u][:, :, :width], func=ACT.Exp,
+                                 bias=neg_max[u][:, 1:2], scale=-1.0, accum_out=row_sums[pair][:, column:column + 1])
 
         def flip(c, i):
-            for side, banks in ((0, own_bank), (1, prev_bank)):
-                if side == 1 and c == 0:
-                    continue
-                banks[(c, i)] = psum.tile([P, HEADS, 2, P], F32, tag="bank", name="flip_bank")
+            if c > 0:
+                prev_bank[(c, i)] = psum.tile([P, HEADS, 2, P], F32, tag="bank", name="prev_bank")
                 for h in range(HEADS):
-                    words = e_rows[(i, h)][:].bitcast(F32)
+                    into, first_own, first_prev = place(i, h)
                     for u in range(2):
-                        first = ((1 - side) * 2 + u) * P
-                        nc.tensor.transpose(banks[(c, i)][:, h, u, :], words[:, first:first + P], ident_f32[:])
+                        nc.tensor.transpose(prev_bank[(c, i)][:, h, u, :],
+                                            into[:, u, first_prev:first_prev + half].bitcast(F32), ident_f32[:])
+            if i > 0:
+                sets = 1 if i == 1 else HEADS
+                own_bank[(c, i)] = psum.tile([P, sets, 2, P], F32, tag="bank", name="own_bank")
+                for h in range(sets):
+                    for u in range(2):
+                        nc.tensor.transpose(own_bank[(c, i)][:, h, u, :],
+                                            rows[(i, h)][:, u, half:2 * half].bitcast(F32), ident_f32[:])
 
         def regroup(c, i):
-            e_grp[(c, i)] = work.tile([P, 2 * HEADS * CHUNK], BF16, align_bytes=64, bufs=3, name="e_grp")
-            grouped = e_grp[(c, i)][:].bitcast(F32).rearrange("p (s h x u) -> p s h x u", s=2, h=HEADS, u=2)
-            own_words = own_bank[(c, i)][:].rearrange("p h u x -> p h x u")
-            if i % 2 == 0:
-                nc.vector.tensor_copy(out=grouped[:, 0], in_=own_words)
-            else:
-                nc.scalar.copy(out=grouped[:, 0], in_=own_words)
+            e_grp[(c, i)] = work.tile([P, 2, HEADS * CHUNK], BF16, align_bytes=64, bufs=3, name="e_grp")
+            if i > 0:
+                sets = 1 if i == 1 else HEADS
+                grouped = e_grp[(c, i)][:, 0, :sets * CHUNK].bitcast(F32).rearrange("p (h x u) -> p h x u", h=sets, u=2)
+                words = own_bank[(c, i)][:].rearrange("p h u x -> p h x u")
+                if i in OWN_ON_SCALAR:
+                    nc.scalar.copy(out=grouped, in_=words)
+                else:
+                    nc.vector.tensor_copy(out=grouped, in_=words)
             if c > 0:
-                nc.scalar.copy(out=grouped[:, 1], in_=prev_bank[(c, i)][:].rearrange("p h u x -> p h x u"))
+                nc.scalar.copy(
+                    out=e_grp[(c, i)][:, 1, :].bitcast(F32).rearrange("p (h x u) -> p h x u", h=HEADS, u=2),
+                    in_=prev_bank[(c, i)][:].rearrange("p h u x -> p h x u"),
+                )
 
         def quantise(c, i):
-            sides = 1 if c == 0 else 2
-            e_codes[(c, i)] = work.tile([P, 2 * HEADS * P], U32, align_bytes=64, bufs=3, name="e_codes")
-            e_scales[(c, i)] = work.tile([P, 2 * HEADS * P], U8, align_bytes=64, bufs=3, name="e_scales")
-            nc.vector.quantize_mx(
-                out=e_codes[(c, i)][:, :sides * HEADS * P].bitcast(FP8X4), scales=e_scales[(c, i)][:, :sides * HEADS * P],
-                in_=e_grp[(c, i)][:, :sides * HEADS * CHUNK],
-            )
+            e_codes[(c, i)] = work.tile([P, 2 * HEADS * P], U32, align_bytes=64, bufs=4, name="e_codes")
+            e_scales[(c, i)] = work.tile([P, 2 * HEADS * P], U8, align_bytes=64, bufs=4, name="e_scales")
+            own = 0 if i == 0 else (1 if i == 1 else HEADS) * P
+            before = HEADS * P if c > 0 else 0
+            if own == HEADS * P and before:
+                parts = ((0, own + before),)
+            else:
+                parts = ((0, own), (HEADS * P, before))
+            grouped = e_grp[(c, i)][:].rearrange("p s y -> p (s y)")
+            for first, words in parts:
+                if words:
+                    nc.vector.quantize_mx(
+                        out=e_codes[(c, i)][:, first:first + words].bitcast(FP8X4),
+                        scales=e_scales[(c, i)][:, first:first + words],
+                        in_=grouped[:, first * PACK:(first + words) * PACK],
+                    )
 
         def weighted_sum(c, i):
-            if i % 2 == 0:
-                acc[(c, i // 2)] = psum_sum.tile([P, 2, HEADS, DH], F32, name="acc")
+            if i < 2:
+                acc[(c, i % 2)] = psum_sum.tile([P, 2, HEADS, DH], F32, name="acc")
+            b = c % 2
             for h in range(HEADS):
-                for side in range(1 if c == 0 else 2):
-                    queries = slice((side * HEADS + h) * P, (side * HEADS + h + 1) * P)
-                    features = slice(h * DH, (h + 1) * DH)
+                features = slice(h * DH, (h + 1) * DH)
+                source = (c, 2 if i == 0 else i)
+                first = 0 if i == 1 else h * P
+                codes, scales = v_codes[c][:, features], v_scales[c][:, features]
+                if i == 0:
+                    codes, scales = v_back[b][:, features], v_back_scales[b][:, features]
+                elif i == 1:
+                    codes = v_half[b][:, features]
+                    if h == 1:
+                        scales = v_half_scales[b][:]
+                elif i == 2:
+                    codes = v_front[b][:, features]
+                products = [(source, first, codes, scales)]
+                if c > 0:
+                    products.append(((c, i), (HEADS + h) * P, v_codes[c - 1][:, features], v_scales[c - 1][:, features]))
+                for n_done, (source, first, codes, scales) in enumerate(products):
                     nc.tensor.matmul_mx(
-                        out=acc[(c, i // 2)][:, i % 2, h, :],
-                        lhsT=e_codes[(c, i)][:, queries].bitcast(FP8X4), lhsT_scale=e_scales[(c, i)][:, queries],
-                        rhs=v_codes[c - side][:, features].bitcast(FP8X4), rhs_scale=v_scales[c - side][:, features],
-                        start=(side == 0), stop=(side == 1 or c == 0),
+                        out=acc[(c, i % 2)][:, i // 2, h, :],
+                        lhsT=e_codes[source][:, first:first + P].bitcast(FP8X4),
+                        lhsT_scale=e_scales[source][:, first:first + P],
+                        rhs=codes.bitcast(FP8X4), rhs_scale=scales,
+                        start=(n_done == 0), stop=(n_done == len(products) - 1),
                     )
 
         def invert_sums(c, j):
@@ -263,44 +347,70 @@ def tile_localselfattention_pa_t_kernel(tc, q, k_scaled, hidden_states, Wv, out)
                 in0=acc[(c, j)][:].rearrange("p t h d -> p (t h) d"),
                 in1=inverse[(c, j)][:].unsqueeze(2).to_broadcast([P, 2 * HEADS, DH]), op=ALU.mult,
             )
-            nc.sync.dma_start(out=out_rows[c * TILES // 2 + j], in_=result[:])
+            nc.sync.dma_start(out=out_rows[c, j], in_=result[:])
 
-        pieces = TILES + 2 + HEADS
-        assert pieces == TILES * HEADS
         n = len(units)
+
+        def prepare(j, stage):
+            c, piece = j // 8, j % 8
+            if piece < PACK:
+                if j == PACK - 2 and stage == 2:
+                    group_weights()
+                if j == PACK - 1 and stage == 2:
+                    quantise_weights()
+                if 0 <= c < N_CHUNKS:
+                    (transpose_hidden, copy_hidden, quantise_hidden)[stage](c, piece)
+            elif piece < PACK + 2:
+                if 0 <= c + 1 < N_CHUNKS:
+                    name, src = (("k", k_raw), ("q", q_raw))[piece - PACK]
+                    if stage == 0:
+                        transpose_keys_or_queries(c + 1, src[c + 1], name)
+                    elif stage == 1:
+                        copy_keys_or_queries(c + 1, name)
+            elif 0 <= c < N_CHUNKS:
+                h = piece - PACK - 2
+                if stage == 0:
+                    multiply_values(c, h)
+                elif stage == 1:
+                    copy_values(c, h)
+                elif h == HEADS - 1:
+                    quantise_values(c)
+                    spread_values(c)
+                    if c + 2 < N_CHUNKS:
+                        load(c + 2)
 
         def tile_done(u):
             return 0 <= u < n and units[u][2] == HEADS - 1
 
         def pair_done(u):
-            return tile_done(u) and units[u][1] % 2 == 1
+            return tile_done(u) and units[u][1] >= 2
 
         ctx.enter_context(tc.manual_schedule())
-        for k in range(-LEAD, n + 5):
-            if pair_done(k - 5):
-                finish(units[k - 5][0], units[k - 5][1] // 2)
-            if tile_done(k - 4):
-                weighted_sum(units[k - 4][0], units[k - 4][1])
-            if pair_done(k - 3):
-                invert_sums(units[k - 3][0], units[k - 3][1] // 2)
-            if tile_done(k - 3):
-                quantise(units[k - 3][0], units[k - 3][1])
-            if tile_done(k - 2):
-                regroup(units[k - 2][0], units[k - 2][1])
-            if 0 <= k + LEAD - 2 < n:
-                prepare_quantise((k + LEAD - 2) // pieces, (k + LEAD - 2) % pieces)
-            if 0 <= k + LEAD - 1 < n:
-                prepare_copy((k + LEAD - 1) // pieces, (k + LEAD - 1) % pieces)
+        for k in range(-LEAD - 4, n + 7):
             if 0 <= k < n:
-                exponentials(k)
-            if 0 <= k + 1 < n:
-                move_own(k + 1)
+                move_own(k)
             if 0 <= k + 2 < n:
                 move_prev(k + 2)
-                scores_own(k + 2)
+            if pair_done(k - 6):
+                finish(units[k - 6][0], units[k - 6][1] % 2)
+            if pair_done(k - 4):
+                invert_sums(units[k - 4][0], units[k - 4][1] % 2)
+            if tile_done(k - 4):
+                quantise(units[k - 4][0], units[k - 4][1])
+            prepare(k + LEAD - 2, 2)
+            if 0 <= k - 1 < n:
+                exponentials(k - 1)
+            if tile_done(k - 3):
+                regroup(units[k - 3][0], units[k - 3][1])
+            prepare(k + LEAD - 1, 1)
+            if 0 <= k + 1 < n:
+                scores_own(k + 1)
             if 0 <= k + 3 < n:
                 scores_prev(k + 3)
-            if tile_done(k - 1):
-                flip(units[k - 1][0], units[k - 1][1])
-            if 0 <= k + LEAD < n:
-                prepare_on_tensor((k + LEAD) // pieces, (k + LEAD) % pieces)
+            if tile_done(k - 5):
+                c, i, h = units[k - 5]
+                for tile in {0: (), 2: (0, 2), 1: (1,), 3: (3,)}[i]:
+                    weighted_sum(c, tile)
+            if tile_done(k - 2):
+                flip(units[k - 2][0], units[k - 2][1])
+            prepare(k + LEAD, 0)

@@ -49,6 +49,11 @@ def tile_localselfattention_pa_t_kernel(tc, q, k_scaled, hidden_states, Wv, out)
         q_raw, k_raw, h_raw = {}, {}, {}
         w_raw = raw.tile([P, HID_PASSES * PACK * WIDTH], BF16)
 
+        def keep_busy(count):
+            bank = psum_sum.tile([P, CHUNK], F32, tag="acc", name="unread")
+            for j in range(count):
+                nc.tensor.matmul(bank[:], lhsT=zeros[:, :P], rhs=zeros[:], start=True, stop=True)
+
         def load(c):
             k_raw[c] = raw.tile([P, PACK, WIDTH], BF16, name="k_raw%d" % c)
             nc.sync.dma_start(out=k_raw[c][:], in_=k_rows[c])
@@ -67,6 +72,9 @@ def tile_localselfattention_pa_t_kernel(tc, q, k_scaled, hidden_states, Wv, out)
         load(0)
         load(1)
 
+        zeros = const.tile([P, CHUNK], BF16)
+        nc.vector.memset(zeros[:], 0.0)
+        keep_busy(4)
         ident_bf = const.tile([P, P], BF16)
         make_identity(nc, ident_bf[:])
         ident_f32 = const.tile([P, P], F32)
@@ -208,6 +216,8 @@ def tile_localselfattention_pa_t_kernel(tc, q, k_scaled, hidden_states, Wv, out)
             seen = (i + 1) * P // PACK
             queries = q_t[c][:, h, i, :]
             s_own[u] = psum_scores.tile([P, CHUNK], F32, tag="own", name="s_own")
+            if i == 0:
+                nc.tensor.matmul(s_own[u][:], lhsT=ident_bf[:], rhs=k_t[c][:, h, :, :], start=True, stop=True)
             scores = s_own[u][:, :PACK * seen].rearrange("p (t x) -> p t x", t=PACK)
             nc.tensor.matmul(scores, lhsT=queries, rhs=k_t[c][:, h, :, :seen], start=True, stop=False)
             nc.tensor.matmul(scores[:, :, seen - P // PACK:], lhsT=ident_bf[:], rhs=mask_bf[:], start=False, stop=True)
@@ -309,7 +319,7 @@ def tile_localselfattention_pa_t_kernel(tc, q, k_scaled, hidden_states, Wv, out)
 
         def weighted_sum(c, i):
             if i < 2:
-                acc[(c, i % 2)] = psum_sum.tile([P, 2, HEADS, DH], F32, name="acc")
+                acc[(c, i % 2)] = psum_sum.tile([P, 2, HEADS, DH], F32, tag="acc", name="acc")
             b = c % 2
             for h in range(HEADS):
                 features = slice(h * DH, (h + 1) * DH)
@@ -387,6 +397,8 @@ def tile_localselfattention_pa_t_kernel(tc, q, k_scaled, hidden_states, Wv, out)
 
         ctx.enter_context(tc.manual_schedule())
         for k in range(-LEAD - 4, n + 7):
+            if -6 <= k <= 0:
+                keep_busy(1)
             if 0 <= k < n:
                 move_own(k)
             if 0 <= k + 2 < n:

@@ -24,7 +24,7 @@ N_CHUNKS = SEQ // CHUNK
 TILES = CHUNK // P
 HID_PASSES = HID // CHUNK
 MASKED = -1.0e9
-OWN_ON_SCALAR = (2, 1)
+OWN_ON_SCALAR = ()
 LEAD = 5
 
 SCORE_CELLS = HEADS * (2 * N_CHUNKS - 1) * CHUNK * CHUNK

@@ -24,7 +24,8 @@ N_CHUNKS = SEQ // CHUNK
 TILES = CHUNK // P
 HID_PASSES = HID // CHUNK
 MASKED = -1.0e9
-OWN_ON_SCALAR = ()
+OWN_ON_SCALAR = (1,)
+LOADS_AHEAD = 3
 LEAD = 5
 
 SCORE_CELLS = HEADS * (2 * N_CHUNKS - 1) * CHUNK * CHUNK
@@ -69,8 +70,8 @@ def tile_localselfattention_pa_t_kernel(tc, q, k_scaled, hidden_states, Wv, out)
                     in_=Wv.rearrange("(s p e) n -> p s (e n)", p=P, e=2),
                 )
 
-        load(0)
-        load(1)
+        for c in range(LOADS_AHEAD):
+            load(c)
 
         zeros = const.tile([P, CHUNK], BF16)
         nc.vector.memset(zeros[:], 0.0)
@@ -386,8 +387,8 @@ def tile_localselfattention_pa_t_kernel(tc, q, k_scaled, hidden_states, Wv, out)
                 elif h == HEADS - 1:
                     quantise_values(c)
                     spread_values(c)
-                    if c + 2 < N_CHUNKS:
-                        load(c + 2)
+                    if c + LOADS_AHEAD < N_CHUNKS:
+                        load(c + LOADS_AHEAD)
 
         def tile_done(u):
             return 0 <= u < n and units[u][2] == HEADS - 1

@@ -24,7 +24,6 @@ N_CHUNKS = SEQ // CHUNK
 TILES = CHUNK // P
 HID_PASSES = HID // CHUNK
 MASKED = -1.0e9
-OWN_ON_SCALAR = (1,)
 LOADS_AHEAD = 3
 LEAD = 5
 
@@ -75,7 +74,7 @@ def tile_localselfattention_pa_t_kernel(tc, q, k_scaled, hidden_states, Wv, out)
 
         zeros = const.tile([P, CHUNK], BF16)
         nc.vector.memset(zeros[:], 0.0)
-        keep_busy(4)
+        keep_busy(5)
         ident_bf = const.tile([P, P], BF16)
         make_identity(nc, ident_bf[:])
         ident_f32 = const.tile([P, P], F32)
@@ -290,7 +289,7 @@ def tile_localselfattention_pa_t_kernel(tc, q, k_scaled, hidden_states, Wv, out)
                 sets = 1 if i == 1 else HEADS
                 grouped = e_grp[(c, i)][:, 0, :sets * CHUNK].bitcast(F32).rearrange("p (h x u) -> p h x u", h=sets, u=2)
                 words = own_bank[(c, i)][:].rearrange("p h u x -> p h x u")
-                if i in OWN_ON_SCALAR:
+                if i == 1 or c == 0 or (c == N_CHUNKS - 1 and i == 2):
                     nc.scalar.copy(out=grouped, in_=words)
                 else:
                     nc.vector.tensor_copy(out=grouped, in_=words)
@@ -398,7 +397,7 @@ def tile_localselfattention_pa_t_kernel(tc, q, k_scaled, hidden_states, Wv, out)
 
         ctx.enter_context(tc.manual_schedule())
         for k in range(-LEAD - 4, n + 7):
-            if -6 <= k <= 0:
+            if -6 <= k < 0:
                 keep_busy(1)
             if 0 <= k < n:
                 move_own(k)

@@ -216,8 +216,6 @@ def tile_localselfattention_pa_t_kernel(tc, q, k_scaled, hidden_states, Wv, out)
             seen = (i + 1) * P // PACK
             queries = q_t[c][:, h, i, :]
             s_own[u] = psum_scores.tile([P, CHUNK], F32, tag="own", name="s_own")
-            if i == 0:
-                nc.tensor.matmul(s_own[u][:], lhsT=ident_bf[:], rhs=k_t[c][:, h, :, :], start=True, stop=True)
             scores = s_own[u][:, :PACK * seen].rearrange("p (t x) -> p t x", t=PACK)
             nc.tensor.matmul(scores, lhsT=queries, rhs=k_t[c][:, h, :, :seen], start=True, stop=False)
             nc.tensor.matmul(scores[:, :, seen - P // PACK:], lhsT=ident_bf[:], rhs=mask_bf[:], start=False, stop=True)

@@ -25,7 +25,7 @@ TILES = CHUNK // P
 HID_PASSES = HID // CHUNK
 MASKED = -1.0e9
 LOADS_AHEAD = 3
-LEAD = 5
+LEAD = 2
 
 SCORE_CELLS = HEADS * (2 * N_CHUNKS - 1) * CHUNK * CHUNK
 FLOPS = 2 * SEQ * HID * WIDTH + 2 * 2 * SCORE_CELLS * DH
@@ -42,8 +42,8 @@ def tile_localselfattention_pa_t_kernel(tc, q, k_scaled, hidden_states, Wv, out)
         const = ctx.enter_context(tc.tile_pool(name="const", bufs=1))
         raw = ctx.enter_context(tc.tile_pool(name="raw", bufs=1))
         work = ctx.enter_context(tc.tile_pool(name="work", bufs=2))
-        psum = ctx.enter_context(tc.psum_pool(name="psum", bufs=3))
-        psum_scores = ctx.enter_context(tc.psum_pool(name="psum_scores", bufs=2))
+        psum = ctx.enter_context(tc.psum_pool(name="psum", bufs=4))
+        psum_scores = ctx.enter_context(tc.psum_pool(name="psum_scores", bufs=3))
         psum_sum = ctx.enter_context(tc.psum_pool(name="psum_sum", bufs=1))
 
         q_raw, k_raw, h_raw = {}, {}, {}
@@ -74,7 +74,7 @@ def tile_localselfattention_pa_t_kernel(tc, q, k_scaled, hidden_states, Wv, out)
 
         zeros = const.tile([P, CHUNK], BF16)
         nc.vector.memset(zeros[:], 0.0)
-        keep_busy(5)
+        keep_busy(3)
         ident_bf = const.tile([P, P], BF16)
         make_identity(nc, ident_bf[:])
         ident_f32 = const.tile([P, P], F32)
@@ -162,7 +162,7 @@ def tile_localselfattention_pa_t_kernel(tc, q, k_scaled, hidden_states, Wv, out)
         def copy_keys_or_queries(c, name):
             into, bufs = (k_t, 3) if name == "k" else (q_t, 2)
             into[c] = work.tile([P, HEADS, TILES, P], BF16, tag=name + "_t", bufs=bufs, name="turned")
-            nc.scalar.copy(out=into[c][:], in_=prep_bank[(c, name)][:])
+            nc.vector.tensor_copy(out=into[c][:], in_=prep_bank[(c, name)][:])
 
         def copy_hidden(c, t):
             if t == 0:
@@ -215,7 +215,7 @@ def tile_localselfattention_pa_t_kernel(tc, q, k_scaled, hidden_states, Wv, out)
             c, i, h = units[u]
             seen = (i + 1) * P // PACK
             queries = q_t[c][:, h, i, :]
-            s_own[u] = psum_scores.tile([P, CHUNK], F32, tag="own", name="s_own")
+            s_own[u] = psum_scores.tile([P, CHUNK], F32, tag="bank", name="s_own")
             scores = s_own[u][:, :PACK * seen].rearrange("p (t x) -> p t x", t=PACK)
             nc.tensor.matmul(scores, lhsT=queries, rhs=k_t[c][:, h, :, :seen], start=True, stop=False)
             nc.tensor.matmul(scores[:, :, seen - P // PACK:], lhsT=ident_bf[:], rhs=mask_bf[:], start=False, stop=True)
@@ -223,7 +223,7 @@ def tile_localselfattention_pa_t_kernel(tc, q, k_scaled, hidden_states, Wv, out)
         def scores_prev(u):
             c, i, h = units[u]
             if c > 0:
-                s_prev[u] = psum_scores.tile([P, PACK, P], F32, tag="prev", name="s_prev")
+                s_prev[u] = psum_scores.tile([P, PACK, P], F32, tag="bank", name="s_prev")
                 nc.tensor.matmul(s_prev[u][:], lhsT=q_t[c][:, h, i, :], rhs=k_t[c - 1][:, h, :, :], start=True, stop=True)
 
         def move(u, scores, column, initial, result):
@@ -243,8 +243,8 @@ def tile_localselfattention_pa_t_kernel(tc, q, k_scaled, hidden_states, Wv, out)
             return (0, own, own + half) if first_own < first_prev else (half, 0, own + half)
 
         def move_prev(u):
-            neg_scores[u] = work.tile([P, 2, CHUNK], F32, bufs=5, name="neg_scores")
-            neg_max[u] = work.tile([P, 2], F32, bufs=6, name="neg_max")
+            neg_scores[u] = work.tile([P, 2, CHUNK], F32, bufs=6, name="neg_scores")
+            neg_max[u] = work.tile([P, 2], F32, bufs=8, name="neg_max")
             if units[u][0] > 0:
                 move(u, s_prev[u][:], columns(u)[1], None, neg_max[u][:, 0:1])
 
@@ -257,7 +257,7 @@ def tile_localselfattention_pa_t_kernel(tc, q, k_scaled, hidden_states, Wv, out)
             c, i, h = units[u]
             pair = (c, i % 2)
             if i < 2 and h == 0:
-                row_sums[pair] = work.tile([P, 2 * HEADS], F32, bufs=3, name="row_sums")
+                row_sums[pair] = work.tile([P, 2 * HEADS], F32, bufs=4, name="row_sums")
             into, first_own, first_prev = place(i, h)
             first = first_own if c == 0 else min(first_own, first_prev)
             width = columns(u)[2]
@@ -287,10 +287,7 @@ def tile_localselfattention_pa_t_kernel(tc, q, k_scaled, hidden_states, Wv, out)
                 sets = 1 if i == 1 else HEADS
                 grouped = e_grp[(c, i)][:, 0, :sets * CHUNK].bitcast(F32).rearrange("p (h x u) -> p h x u", h=sets, u=2)
                 words = own_bank[(c, i)][:].rearrange("p h u x -> p h x u")
-                if i == 1 or c == 0 or (c == N_CHUNKS - 1 and i == 2):
-                    nc.scalar.copy(out=grouped, in_=words)
-                else:
-                    nc.vector.tensor_copy(out=grouped, in_=words)
+                nc.scalar.copy(out=grouped, in_=words)
             if c > 0:
                 nc.scalar.copy(
                     out=e_grp[(c, i)][:, 1, :].bitcast(F32).rearrange("p (h x u) -> p h x u", h=HEADS, u=2),
@@ -394,33 +391,33 @@ def tile_localselfattention_pa_t_kernel(tc, q, k_scaled, hidden_states, Wv, out)
             return tile_done(u) and units[u][1] >= 2
 
         ctx.enter_context(tc.manual_schedule())
-        for k in range(-LEAD - 4, n + 7):
-            if -6 <= k < 0:
+        for k in range(-LEAD - 4, n + 11):
+            if -3 <= k < 3:
                 keep_busy(1)
             if 0 <= k < n:
                 move_own(k)
-            if 0 <= k + 2 < n:
-                move_prev(k + 2)
-            if pair_done(k - 6):
-                finish(units[k - 6][0], units[k - 6][1] % 2)
-            if pair_done(k - 4):
-                invert_sums(units[k - 4][0], units[k - 4][1] % 2)
-            if tile_done(k - 4):
-                quantise(units[k - 4][0], units[k - 4][1])
-            prepare(k + LEAD - 2, 2)
-            if 0 <= k - 1 < n:
-                exponentials(k - 1)
-            if tile_done(k - 3):
-                regroup(units[k - 3][0], units[k - 3][1])
-            prepare(k + LEAD - 1, 1)
-            if 0 <= k + 1 < n:
-                scores_own(k + 1)
-            if 0 <= k + 3 < n:
-                scores_prev(k + 3)
-            if tile_done(k - 5):
-                c, i, h = units[k - 5]
+            if tile_done(k - 9):
+                c, i, h = units[k - 9]
                 for tile in {0: (), 2: (0, 2), 1: (1,), 3: (3,)}[i]:
                     weighted_sum(c, tile)
+            if 0 <= k - 2 < n:
+                exponentials(k - 2)
             if tile_done(k - 2):
                 flip(units[k - 2][0], units[k - 2][1])
+            prepare(k + LEAD - 2, 1)
+            if 0 <= k + 1 < n:
+                scores_own(k + 1)
+            if tile_done(k - 3):
+                regroup(units[k - 3][0], units[k - 3][1])
+            if 0 <= k + 2 < n:
+                move_prev(k + 2)
+            prepare(k + LEAD - 2, 2)
+            if tile_done(k - 7):
+                quantise(units[k - 7][0], units[k - 7][1])
+            if pair_done(k - 10):
+                finish(units[k - 10][0], units[k - 10][1] % 2)
             prepare(k + LEAD, 0)
+            if 0 <= k + 3 < n:
+                scores_prev(k + 3)
+            if pair_done(k - 5):
+                invert_sums(units[k - 5][0], units[k - 5][1] % 2)

from contextlib import ExitStack

import concourse.mybir as mybir
from concourse.masks import make_identity

F32 = mybir.dt.float32
BF16 = mybir.dt.bfloat16
U32 = mybir.dt.uint32
I32 = mybir.dt.int32
U8 = mybir.dt.uint8
FP8X4 = mybir.dt.float8_e4m3fn_x4
ACT = mybir.ActivationFunctionType
ALU = mybir.AluOpType

P = 128
PACK = 4
SEQ = 4096
HID = 1024
HEADS = 2
DH = 128
WIDTH = HEADS * DH
CHUNK = 512
N_CHUNKS = SEQ // CHUNK
TILES = CHUNK // P
HID_PASSES = HID // CHUNK
MASKED = -1.0e9
LOADS_AHEAD = 3
LEAD = 2

SCORE_CELLS = HEADS * (2 * N_CHUNKS - 1) * CHUNK * CHUNK
FLOPS = 2 * SEQ * HID * WIDTH + 2 * 2 * SCORE_CELLS * DH


def tile_localselfattention_pa_t_kernel(tc, q, k_scaled, hidden_states, Wv, out):
    nc = tc.nc
    q_rows = q.flatten_outer_dims().rearrange("(c i p) w -> c p i w", i=TILES, p=P)
    k_rows = k_scaled.flatten_outer_dims().rearrange("(c p t) w -> c p t w", t=PACK, p=P)
    h_rows = hidden_states.flatten_outer_dims().rearrange("(c p t) k -> c p t k", t=PACK, p=P)
    out_rows = out.flatten_outer_dims().rearrange("(c a b p) w -> c b p a w", a=2, b=2, p=P)

    with ExitStack() as ctx:
        const = ctx.enter_context(tc.tile_pool(name="const", bufs=1))
        raw = ctx.enter_context(tc.tile_pool(name="raw", bufs=1))
        work = ctx.enter_context(tc.tile_pool(name="work", bufs=2))
        psum = ctx.enter_context(tc.psum_pool(name="psum", bufs=4))
        psum_scores = ctx.enter_context(tc.psum_pool(name="psum_scores", bufs=3))
        psum_sum = ctx.enter_context(tc.psum_pool(name="psum_sum", bufs=1))

        q_raw, k_raw, h_raw = {}, {}, {}
        w_raw = raw.tile([P, HID_PASSES * PACK * WIDTH], BF16)

        def keep_busy(count):
            bank = psum_sum.tile([P, CHUNK], F32, tag="acc", name="unread")
            for j in range(count):
                nc.tensor.matmul(bank[:], lhsT=zeros[:, :P], rhs=zeros[:], start=True, stop=True)

        def load(c):
            k_raw[c] = raw.tile([P, PACK, WIDTH], BF16, name="k_raw%d" % c)
            nc.sync.dma_start(out=k_raw[c][:], in_=k_rows[c])
            q_raw[c] = raw.tile([P, TILES, WIDTH], BF16, name="q_raw%d" % c)
            nc.sync.dma_start(out=q_raw[c][:], in_=q_rows[c])
            h_raw[c] = raw.tile([P, PACK * HID], BF16, name="h_raw%d" % c)
            for t in range(0, PACK, 2):
                nc.sync.dma_start(out=h_raw[c][:, t * HID:(t + 2) * HID].rearrange("p (t k) -> p t k", t=2),
                                  in_=h_rows[c][:, t:t + 2, :])
            if c == 0:
                nc.sync.dma_start(
                    out=w_raw[:].rearrange("p (s x) -> p s x", s=HID_PASSES * 2),
                    in_=Wv.rearrange("(s p e) n -> p s (e n)", p=P, e=2),
                )

        for c in range(LOADS_AHEAD):
            load(c)

        zeros = const.tile([P, CHUNK], BF16)
        nc.vector.memset(zeros[:], 0.0)
        keep_busy(3)
        ident_bf = const.tile([P, P], BF16)
        make_identity(nc, ident_bf[:])
        ident_f32 = const.tile([P, P], F32)
        make_identity(nc, ident_f32[:])
        mask_f32 = const.tile([P, P], F32)
        nc.gpsimd.memset(mask_f32[:], 0.0)
        nc.gpsimd.affine_select(
            out=mask_f32[:], in_=mask_f32[:], compare_op=ALU.is_ge, fill=MASKED,
            base=0, pattern=[[-1, P]], channel_multiplier=1,
        )
        mask_bf = const.tile([P, PACK, P // PACK], BF16)
        nc.vector.tensor_copy(out=mask_bf[:], in_=mask_f32[:].rearrange("p (x t) -> p t x", t=PACK))

        half = CHUNK // 2
        rows = {}
        for i, h, width in ((2, 0, 3 * half), (2, 1, 3 * half), (1, 0, 3 * half), (3, 0, 2 * half), (3, 1, 2 * half)):
            rows[(i, h)] = const.tile([P, 2, width], BF16, align_bytes=64, name="rows_%d_%d" % (i, h))

        def place(i, h):
            own = (i + 1) * P // 2
            if i == 0:
                return rows[(2, h)], 2 * half - own, 2 * half
            if i == 1 and h == 1:
                return rows[(1, 0)], 2 * half - own, 2 * half
            return rows[(i, h)], half, 0

        v_front, v_back, v_half, v_back_scales, v_half_scales = {}, {}, {}, {}, {}
        for b in range(2):
            v_front[b] = const.tile([P, WIDTH], U32, align_bytes=64, name="v_front%d" % b)
            v_back[b] = const.tile([P, WIDTH], U32, align_bytes=64, name="v_back%d" % b)
            v_half[b] = const.tile([P, WIDTH], U32, align_bytes=64, name="v_half%d" % b)
            v_back_scales[b] = const.tile([P, WIDTH], U8, align_bytes=64, name="v_back_scales%d" % b)
            v_half_scales[b] = const.tile([P, DH], U8, align_bytes=64, name="v_half_scales%d" % b)
            for t in (v_front[b], v_back[b], v_half[b]):
                nc.gpsimd.memset(t[:], 0)
            for t in (v_back_scales[b], v_half_scales[b]):
                nc.gpsimd.memset(t[:].bitcast(I32), 0)

        w_grp = const.tile([P, HID_PASSES * WIDTH * PACK], BF16, align_bytes=64)
        w_codes = const.tile([P, HID_PASSES * WIDTH], U32, align_bytes=64)
        w_scales = const.tile([P, HID_PASSES * WIDTH], U8, align_bytes=64)

        def group_weights():
            nc.vector.tensor_copy(
                out=w_grp[:].rearrange("p (g n t) -> p g n t", g=HID_PASSES, t=PACK),
                in_=w_raw[:].rearrange("p (g t n) -> p g n t", g=HID_PASSES, t=PACK),
            )

        def quantise_weights():
            nc.vector.quantize_mx(out=w_codes[:].bitcast(FP8X4), scales=w_scales[:], in_=w_grp[:])

        k_t, q_t, h_grp, h_codes, h_scales, v_grp, v_codes, v_scales = {}, {}, {}, {}, {}, {}, {}, {}
        prep_bank = {}

        def transpose_keys_or_queries(c, src, name):
            bank = psum.tile([P, HEADS, TILES, P], BF16, tag="bank", name="qk_bank")
            for h in range(HEADS):
                for i in range(TILES):
                    nc.tensor.transpose(bank[:, h, i, :], src[:, i, h * DH:(h + 1) * DH], ident_bf[:])
            prep_bank[(c, name)] = bank

        def transpose_hidden(c, t):
            words = h_raw[c][:].bitcast(F32)
            bank = psum.tile([P, HID_PASSES, 2, P], F32, tag="bank", name="h_bank")
            for g in range(HID_PASSES):
                for a in range(2):
                    first = (t * HID_PASSES * 2 + g * 2 + a) * P
                    nc.tensor.transpose(bank[:, g, a, :], words[:, first:first + P], ident_f32[:])
            prep_bank[(c, "h", t)] = bank

        def multiply_values(c, h):
            bank = psum.tile([P, PACK, DH], F32, tag="bank", name="v_bank")
            for t in range(PACK):
                for g in range(HID_PASSES):
                    r = slice((t * HID_PASSES + g) * P, (t * HID_PASSES + g + 1) * P)
                    cols = slice(g * WIDTH + h * DH, g * WIDTH + (h + 1) * DH)
                    nc.tensor.matmul_mx(
                        out=bank[:, t, :],
                        lhsT=h_codes[c][:, r].bitcast(FP8X4), lhsT_scale=h_scales[c][:, r],
                        rhs=w_codes[:, cols].bitcast(FP8X4), rhs_scale=w_scales[:, cols],
                        start=(g == 0), stop=(g == HID_PASSES - 1),
                    )
            prep_bank[(c, "v", h)] = bank

        def copy_keys_or_queries(c, name):
            into, bufs = (k_t, 3) if name == "k" else (q_t, 2)
            into[c] = work.tile([P, HEADS, TILES, P], BF16, tag=name + "_t", bufs=bufs, name="turned")
            nc.vector.tensor_copy(out=into[c][:], in_=prep_bank[(c, name)][:])

        def copy_hidden(c, t):
            if t == 0:
                h_grp[c] = work.tile([P, PACK * HID_PASSES * P * PACK], BF16, align_bytes=64, name="h_grp")
            grouped = h_grp[c][:].bitcast(F32).rearrange("p (t g x a) -> p t g x a", t=PACK, g=HID_PASSES, a=2)
            nc.scalar.copy(out=grouped[:, t], in_=prep_bank[(c, "h", t)][:].rearrange("p g a x -> p g x a"))

        def copy_values(c, h):
            if h == 0:
                v_grp[c] = work.tile([P, WIDTH * PACK], BF16, align_bytes=64, name="v_grp")
            nc.scalar.copy(
                out=v_grp[c][:, h * DH * PACK:(h + 1) * DH * PACK].rearrange("p (d t) -> p d t", t=PACK),
                in_=prep_bank[(c, "v", h)][:].rearrange("p t d -> p d t"),
            )

        def quantise_hidden(c, t):
            if t == 0:
                h_codes[c] = work.tile([P, PACK * HID_PASSES * P], U32, align_bytes=64, name="h_codes")
                h_scales[c] = work.tile([P, PACK * HID_PASSES * P], U8, align_bytes=64, name="h_scales")
            words = slice(t * HID_PASSES * P, (t + 1) * HID_PASSES * P)
            nc.vector.quantize_mx(
                out=h_codes[c][:, words].bitcast(FP8X4), scales=h_scales[c][:, words],
                in_=h_grp[c][:, t * HID_PASSES * P * PACK:(t + 1) * HID_PASSES * P * PACK],
            )

        def quantise_values(c):
            v_codes[c] = work.tile([P, WIDTH], U32, align_bytes=64, bufs=3, name="v_codes")
            v_scales[c] = work.tile([P, WIDTH], U8, align_bytes=64, bufs=3, name="v_scales")
            nc.vector.quantize_mx(out=v_codes[c][:].bitcast(FP8X4), scales=v_scales[c][:], in_=v_grp[c][:])

        def spread_values(c):
            b = c % 2
            codes, scales = v_codes[c], v_scales[c]
            for dst, src in (
                (v_front[b][:96, :], codes[:96, :]),
                (v_back[b][96:, :], codes[:32, :]),
                (v_back_scales[b][96:100, :], scales[0:4, :]),
                (v_half[b][:64, :DH], codes[:64, :DH]),
                (v_half[b][64:, DH:], codes[:64, DH:]),
                (v_half_scales[b][64:68, :], scales[0:4, DH:]),
                (v_half_scales[b][96:100, :], scales[32:36, DH:]),
            ):
                nc.sync.dma_start(out=dst.bitcast(I32), in_=src.bitcast(I32))

        units = [(c, i, h) for c in range(N_CHUNKS) for i in (0, 2, 1, 3) for h in range(HEADS)]
        s_own, s_prev, neg_scores, neg_max, own_bank, prev_bank, e_grp, e_codes, e_scales = {}, {}, {}, {}, {}, {}, {}, {}, {}
        row_sums, inverse, acc = {}, {}, {}

        def scores_own(u):
            c, i, h = units[u]
            seen = (i + 1) * P // PACK
            queries = q_t[c][:, h, i, :]
            s_own[u] = psum_scores.tile([P, CHUNK], F32, tag="bank", name="s_own")
            scores = s_own[u][:, :PACK * seen].rearrange("p (t x) -> p t x", t=PACK)
            nc.tensor.matmul(scores, lhsT=queries, rhs=k_t[c][:, h, :, :seen], start=True, stop=False)
            nc.tensor.matmul(scores[:, :, seen - P // PACK:], lhsT=ident_bf[:], rhs=mask_bf[:], start=False, stop=True)

        def scores_prev(u):
            c, i, h = units[u]
            if c > 0:
                s_prev[u] = psum_scores.tile([P, PACK, P], F32, tag="bank", name="s_prev")
                nc.tensor.matmul(s_prev[u][:], lhsT=q_t[c][:, h, i, :], rhs=k_t[c - 1][:, h, :, :], start=True, stop=True)

        def move(u, scores, column, initial, result):
            seen = scores.shape[2]
            nc.vector.tensor_scalar(
                out=neg_scores[u][:, :, column:column + 2 * seen].rearrange("p u (x e) -> p u x e", e=2),
                in0=scores.rearrange("p (u e) x -> p u x e", e=2),
                scalar1=-1.0, scalar2=initial, op0=ALU.mult, op1=ALU.min, accum_out=result,
            )

        def columns(u):
            c, i, h = units[u]
            own = (i + 1) * P // 2
            first_own, first_prev = place(i, h)[1:]
            if c == 0:
                return 0, None, own
            return (0, own, own + half) if first_own < first_prev else (half, 0, own + half)

        def move_prev(u):
            neg_scores[u] = work.tile([P, 2, CHUNK], F32, bufs=6, name="neg_scores")
            neg_max[u] = work.tile([P, 2], F32, bufs=8, name="neg_max")
            if units[u][0] > 0:
                move(u, s_prev[u][:], columns(u)[1], None, neg_max[u][:, 0:1])

        def move_own(u):
            c, i, h = units[u]
            scores = s_own[u][:, :(i + 1) * P].rearrange("p (t x) -> p t x", t=PACK)
            move(u, scores, columns(u)[0], neg_max[u][:, 0:1] if c > 0 else None, neg_max[u][:, 1:2])

        def exponentials(u):
            c, i, h = units[u]
            pair = (c, i % 2)
            if i < 2 and h == 0:
                row_sums[pair] = work.tile([P, 2 * HEADS], F32, bufs=4, name="row_sums")
            into, first_own, first_prev = place(i, h)
            first = first_own if c == 0 else min(first_own, first_prev)
            width = columns(u)[2]
            column = (i // 2) * HEADS + h
            nc.scalar.activation(out=into[:, :, first:first + width], in_=neg_scores[u][:, :, :width], func=ACT.Exp,
                                 bias=neg_max[u][:, 1:2], scale=-1.0, accum_out=row_sums[pair][:, column:column + 1])

        def flip(c, i):
            if c > 0:
                prev_bank[(c, i)] = psum.tile([P, HEADS, 2, P], F32, tag="bank", name="prev_bank")
                for h in range(HEADS):
                    into, first_own, first_prev = place(i, h)
                    for u in range(2):
                        nc.tensor.transpose(prev_bank[(c, i)][:, h, u, :],
                                            into[:, u, first_prev:first_prev + half].bitcast(F32), ident_f32[:])
            if i > 0:
                sets = 1 if i == 1 else HEADS
                own_bank[(c, i)] = psum.tile([P, sets, 2, P], F32, tag="bank", name="own_bank")
                for h in range(sets):
                    for u in range(2):
                        nc.tensor.transpose(own_bank[(c, i)][:, h, u, :],
                                            rows[(i, h)][:, u, half:2 * half].bitcast(F32), ident_f32[:])

        def regroup(c, i):
            e_grp[(c, i)] = work.tile([P, 2, HEADS * CHUNK], BF16, align_bytes=64, bufs=3, name="e_grp")
            if i > 0:
                sets = 1 if i == 1 else HEADS
                grouped = e_grp[(c, i)][:, 0, :sets * CHUNK].bitcast(F32).rearrange("p (h x u) -> p h x u", h=sets, u=2)
                words = own_bank[(c, i)][:].rearrange("p h u x -> p h x u")
                nc.scalar.copy(out=grouped, in_=words)
            if c > 0:
                nc.scalar.copy(
                    out=e_grp[(c, i)][:, 1, :].bitcast(F32).rearrange("p (h x u) -> p h x u", h=HEADS, u=2),
                    in_=prev_bank[(c, i)][:].rearrange("p h u x -> p h x u"),
                )

        def quantise(c, i):
            e_codes[(c, i)] = work.tile([P, 2 * HEADS * P], U32, align_bytes=64, bufs=4, name="e_codes")
            e_scales[(c, i)] = work.tile([P, 2 * HEADS * P], U8, align_bytes=64, bufs=4, name="e_scales")
            own = 0 if i == 0 else (1 if i == 1 else HEADS) * P
            before = HEADS * P if c > 0 else 0
            if own == HEADS * P and before:
                parts = ((0, own + before),)
            else:
                parts = ((0, own), (HEADS * P, before))
            grouped = e_grp[(c, i)][:].rearrange("p s y -> p (s y)")
            for first, words in parts:
                if words:
                    nc.vector.quantize_mx(
                        out=e_codes[(c, i)][:, first:first + words].bitcast(FP8X4),
                        scales=e_scales[(c, i)][:, first:first + words],
                        in_=grouped[:, first * PACK:(first + words) * PACK],
                    )

        def weighted_sum(c, i):
            if i < 2:
                acc[(c, i % 2)] = psum_sum.tile([P, 2, HEADS, DH], F32, tag="acc", name="acc")
            b = c % 2
            for h in range(HEADS):
                features = slice(h * DH, (h + 1) * DH)
                source = (c, 2 if i == 0 else i)
                first = 0 if i == 1 else h * P
                codes, scales = v_codes[c][:, features], v_scales[c][:, features]
                if i == 0:
                    codes, scales = v_back[b][:, features], v_back_scales[b][:, features]
                elif i == 1:
                    codes = v_half[b][:, features]
                    if h == 1:
                        scales = v_half_scales[b][:]
                elif i == 2:
                    codes = v_front[b][:, features]
                products = [(source, first, codes, scales)]
                if c > 0:
                    products.append(((c, i), (HEADS + h) * P, v_codes[c - 1][:, features], v_scales[c - 1][:, features]))
                for n_done, (source, first, codes, scales) in enumerate(products):
                    nc.tensor.matmul_mx(
                        out=acc[(c, i % 2)][:, i // 2, h, :],
                        lhsT=e_codes[source][:, first:first + P].bitcast(FP8X4),
                        lhsT_scale=e_scales[source][:, first:first + P],
                        rhs=codes.bitcast(FP8X4), rhs_scale=scales,
                        start=(n_done == 0), stop=(n_done == len(products) - 1),
                    )

        def invert_sums(c, j):
            inverse[(c, j)] = work.tile([P, 2 * HEADS], F32, bufs=3, name="inverse")
            nc.vector.reciprocal(out=inverse[(c, j)][:], in_=row_sums[(c, j)][:])

        def finish(c, j):
            result = work.tile([P, 2, WIDTH], F32, bufs=3, name="result")
            nc.vector.tensor_tensor(
                out=result[:].rearrange("p t (h d) -> p (t h) d", h=HEADS),
                in0=acc[(c, j)][:].rearrange("p t h d -> p (t h) d"),
                in1=inverse[(c, j)][:].unsqueeze(2).to_broadcast([P, 2 * HEADS, DH]), op=ALU.mult,
            )
            nc.sync.dma_start(out=out_rows[c, j], in_=result[:])

        n = len(units)

        def prepare(j, stage):
            c, piece = j // 8, j % 8
            if piece < PACK:
                if j == PACK - 2 and stage == 2:
                    group_weights()
                if j == PACK - 1 and stage == 2:
                    quantise_weights()
                if 0 <= c < N_CHUNKS:
                    (transpose_hidden, copy_hidden, quantise_hidden)[stage](c, piece)
            elif piece < PACK + 2:
                if 0 <= c + 1 < N_CHUNKS:
                    name, src = (("k", k_raw), ("q", q_raw))[piece - PACK]
                    if stage == 0:
                        transpose_keys_or_queries(c + 1, src[c + 1], name)
                    elif stage == 1:
                        copy_keys_or_queries(c + 1, name)
            elif 0 <= c < N_CHUNKS:
                h = piece - PACK - 2
                if stage == 0:
                    multiply_values(c, h)
                elif stage == 1:
                    copy_values(c, h)
                elif h == HEADS - 1:
                    quantise_values(c)
                    spread_values(c)
                    if c + LOADS_AHEAD < N_CHUNKS:
                        load(c + LOADS_AHEAD)

        def tile_done(u):
            return 0 <= u < n and units[u][2] == HEADS - 1

        def pair_done(u):
            return tile_done(u) and units[u][1] >= 2

        ctx.enter_context(tc.manual_schedule())
        for k in range(-LEAD - 4, n + 11):
            if -3 <= k < 3:
                keep_busy(1)
            if 0 <= k < n:
                move_own(k)
            if tile_done(k - 9):
                c, i, h = units[k - 9]
                for tile in {0: (), 2: (0, 2), 1: (1,), 3: (3,)}[i]:
                    weighted_sum(c, tile)
            if 0 <= k - 2 < n:
                exponentials(k - 2)
            if tile_done(k - 2):
                flip(units[k - 2][0], units[k - 2][1])
            prepare(k + LEAD - 2, 1)
            if 0 <= k + 1 < n:
                scores_own(k + 1)
            if tile_done(k - 3):
                regroup(units[k - 3][0], units[k - 3][1])
            if 0 <= k + 2 < n:
                move_prev(k + 2)
            prepare(k + LEAD - 2, 2)
            if tile_done(k - 7):
                quantise(units[k - 7][0], units[k - 7][1])
            if pair_done(k - 10):
                finish(units[k - 10][0], units[k - 10][1] % 2)
            prepare(k + LEAD, 0)
            if 0 <= k + 3 < n:
                scores_prev(k + 3)
            if pair_done(k - 5):
                invert_sums(units[k - 5][0], units[k - 5][1] % 2)
